import numpy as np
import ml_dtypes


def mxq(x, axis, fmt="e4m3"):
    dtype, down = {"e4m3": (ml_dtypes.float8_e4m3fn, 7), "e5m2": (ml_dtypes.float8_e5m2, 14)}[fmt]
    v = np.moveaxis(np.asarray(x, np.float32).astype(ml_dtypes.bfloat16).astype(np.float64), axis, -1)
    blocks = v.reshape(v.shape[:-1] + (-1, 32))
    amax = np.abs(blocks).max(-1, keepdims=True)
    byte = np.maximum(np.where(amax > 0, np.frexp(amax)[1] - 1 + 127, 0) - down, 1)
    scale = np.exp2(byte - 127.0)
    codes = (blocks / scale).astype(np.float32).astype(dtype).astype(np.float64)
    return np.moveaxis((codes * scale).reshape(v.shape), -1, axis)


WIDE = False


def mx_kscale(k):
    if not WIDE:
        return np.ones(k)
    levels = np.array([10, -10, 5, -5, 0])
    a = np.random.permutation(np.resize(levels, k // 512 * 4)).reshape(k // 512, 4)
    idx = np.arange(k)
    return np.exp2(a[idx // 512, idx % 128 // 32])


BF16 = ml_dtypes.bfloat16


def bf(x):
    return np.asarray(x, np.float32).astype(BF16)


def f64(x):
    return np.asarray(x).astype(np.float64)


N, C, D, H, W, GD, GH, GW, FD, FH, FW = 1, 512, 8, 8, 8, 8, 8, 8, 4, 8, 8
V = D * H * W
G = GD * GH * GW
PD, PH, PW = D // GD, H // GH, W // GW


def erf(z):
    a = np.minimum(np.abs(z), 6.0)
    q = 2.0 * a * a
    t = a.copy()
    s = a.copy()
    n = 0
    while np.any(t > 1e-18 * s):
        n += 1
        t = t * q / (2 * n + 1)
        s = s + t
    return np.sign(z) * (2.0 / np.sqrt(np.pi)) * np.exp(-a * a) * s


def gelu(t):
    return 0.5 * t * (1.0 + erf(t / np.sqrt(2.0)))


def block(t, ps):
    n, c, d, h, w = t.shape
    t = t.reshape(n, c, d // ps[0], ps[0], h // ps[1], ps[1], w // ps[2], ps[2])
    return t.transpose(0, 1, 2, 4, 6, 3, 5, 7).reshape(n, c, -1, ps[0] * ps[1] * ps[2])


def unblock(t, gs, ps):
    n, c = t.shape[:2]
    t = t.reshape(n, c, gs[0], gs[1], gs[2], ps[0], ps[1], ps[2]).transpose(0, 1, 2, 5, 3, 6, 4, 7)
    return t.reshape(n, c, gs[0] * ps[0], gs[1] * ps[1], gs[2] * ps[2])


def setup_inputs():
    s = mx_kscale(C)
    return {"x_norm": bf(np.random.standard_normal((N, C, D, H, W)) * s[None, :, None, None, None]),
            "w1_u": bf(np.random.standard_normal((C, C)) / np.sqrt(C) / s[None, :]),
            "b1_u": bf(np.random.standard_normal(C) * 0.3),
            "w2": bf(np.random.standard_normal((G, G)) / np.sqrt(G)),
            "b2": bf(np.random.standard_normal(G) * 0.3)}


def reference(x_norm, w1_u, b1_u, w2, b2):
    z = mxq(f64(w1_u), 1, "e4m3") @ mxq(f64(x_norm).reshape(N, C, V), 1, "e4m3")
    u = gelu(z + f64(b1_u)[None, :, None]).reshape(N, C, D, H, W)
    u = block(u, (PD, PH, PW))
    y = (mxq(f64(w2), 1, "e4m3") @ mxq(u, 2, "e4m3")) + f64(b2)[None, None, :, None]
    return unblock(y, (GD, GH, GW), (PD, PH, PW))

@@ -1,0 +1,140 @@
+from contextlib import ExitStack
+
+import concourse.mybir as mybir
+from concourse.masks import make_identity
+
+F32 = mybir.dt.float32
+BF16 = mybir.dt.bfloat16
+U32 = mybir.dt.uint32
+U8 = mybir.dt.uint8
+FP8X4 = mybir.dt.float8_e4m3fn_x4
+ADD = mybir.AluOpType.add
+GELU = mybir.ActivationFunctionType.Gelu
+
+P = 128
+PACK = 4
+SIZE = P * PACK
+TILES = SIZE // P
+
+FLOPS = 2 * 2 * SIZE * SIZE * SIZE
+
+
+def quantise_weight_rows(nc, weights, psum, identity, rows, codes, scales):
+    natural = weights.tile([P, SIZE], BF16, tag="natural")
+    nc.sync.dma_start(out=natural[:], in_=rows)
+    words = natural[:].bitcast(F32).rearrange("r (p s) -> r s p", s=2)
+    flipped = psum.tile([P, 2, P], F32, tag="bank")
+    for s in range(2):
+        nc.tensor.transpose(out=flipped[:, s, :], in_=words[:, s, :], identity=identity)
+    grouped = weights.tile([P, SIZE], BF16, tag="grouped", align_bytes=64)
+    nc.scalar.copy(
+        out=grouped[:].bitcast(F32).rearrange("p (r s) -> p r s", s=2),
+        in_=flipped[:].rearrange("p s r -> p r s"),
+    )
+    nc.vector.quantize_mx(out=codes.bitcast(FP8X4), scales=scales, in_=grouped[:])
+
+
+def tile_getspatialgatingweights_pa_s_kernel(tc, x_norm, w1_u, b1_u, w2, b2, out):
+    nc = tc.nc
+    x_rows = x_norm.rearrange("n c d h w -> (n c) (d h w)")
+    out_rows = out.rearrange("n c d h w -> (n c) (d h w)")
+
+    with ExitStack() as ctx:
+        keep = ctx.enter_context(tc.tile_pool(name="keep", bufs=1))
+        weights = ctx.enter_context(tc.tile_pool(name="weights", bufs=2 * TILES))
+        stage = ctx.enter_context(tc.tile_pool(name="stage", bufs=TILES))
+        psum_z = ctx.enter_context(tc.psum_pool(name="psum_z", bufs=4))
+        psum = ctx.enter_context(tc.psum_pool(name="psum", bufs=4))
+
+        x_raw = keep.tile([P, PACK, SIZE], BF16)
+        nc.sync.dma_start(out=x_raw[:], in_=x_rows.rearrange("(p j) v -> p j v", j=PACK))
+
+        identity = keep.tile([P, P], F32)
+        make_identity(nc, identity[:])
+        ones = keep.tile([P, P], BF16)
+        nc.vector.memset(ones[:], 1.0)
+        zero_column = keep.tile([P, 1], F32)
+        nc.vector.memset(zero_column[:], 0.0)
+        unused_column = keep.tile([P, 1], F32)
+        nc.scalar.activation(out=unused_column[:], in_=zero_column[:], func=GELU)
+
+        bias_rows = keep.tile([P, 2, SIZE], BF16)
+        nc.vector.memset(bias_rows[:], 0.0)
+        nc.scalar.dma_start(out=bias_rows[0:1, 0, :], in_=b1_u.unsqueeze(0))
+        nc.scalar.dma_start(out=bias_rows[0:1, 1, :], in_=b2.unsqueeze(0))
+        bias_all = keep.tile([P, 2, SIZE], F32)
+        for i in range(2):
+            spread = psum.tile([P, SIZE], F32, tag="bank")
+            nc.tensor.matmul(out=spread[:], lhsT=ones[:], rhs=bias_rows[:, i, :], start=True, stop=True)
+            nc.scalar.copy(out=bias_all[:, i, :], in_=spread[:])
+        b1_all = bias_all[:, 0, :]
+        b2_all = bias_all[:, 1, :]
+
+        x_grouped = keep.tile([P, PACK, P, PACK], BF16, align_bytes=64)
+        x_codes = keep.tile([P, PACK, P], U32, align_bytes=64)
+        x_scales = keep.tile([P, PACK, P], U8, align_bytes=64)
+        x_sorted = x_raw[:].rearrange("p j (q t) -> p t q j", t=PACK)
+        for t in range(PACK):
+            if t < PACK - 1:
+                nc.vector.tensor_copy(out=x_grouped[:, t], in_=x_sorted[:, t])
+            else:
+                nc.scalar.copy(out=x_grouped[:, t], in_=x_sorted[:, t])
+        for t in range(PACK):
+            nc.vector.quantize_mx(
+                out=x_codes[:, t, :].bitcast(FP8X4),
+                scales=x_scales[:, t, :],
+                in_=x_grouped[:, t].rearrange("p q j -> p (q j)"),
+            )
+
+        w1_codes = keep.tile([P, TILES, P], U32, align_bytes=64)
+        w1_scales = keep.tile([P, TILES, P], U8, align_bytes=64)
+        w2_codes = keep.tile([P, TILES, P], U32, align_bytes=64)
+        w2_scales = keep.tile([P, TILES, P], U8, align_bytes=64)
+        for i in range(TILES):
+            quantise_weight_rows(
+                nc, weights, psum, identity[:], w1_u[i * P : (i + 1) * P, :], w1_codes[:, i, :], w1_scales[:, i, :]
+            )
+        for i in range(TILES):
+            quantise_weight_rows(
+                nc, weights, psum, identity[:], w2[i * P : (i + 1) * P, :], w2_codes[:, i, :], w2_scales[:, i, :]
+            )
+
+        u_codes = keep.tile([P, TILES, P], U32, align_bytes=64)
+        u_scales = keep.tile([P, TILES, P], U8, align_bytes=64)
+        for m in range(TILES):
+            k_cols = slice(m * P, (m + 1) * P)
+            z = psum_z.tile([P, PACK, P], F32)
+            for t in range(PACK):
+                nc.tensor.matmul_mx(
+                    out=z[:, t, :],
+                    lhsT=x_codes[:, t, :].bitcast(FP8X4),
+                    lhsT_scale=x_scales[:, t, :],
+                    rhs=w1_codes[:, m, :].bitcast(FP8X4),
+                    rhs_scale=w1_scales[:, m, :],
+                    start=True,
+                    stop=True,
+                )
+            biased = stage.tile([P, P, PACK], F32, tag="biased")
+            nc.vector.tensor_tensor(
+                out=biased[:],
+                in0=z[:].rearrange("q t k -> q k t"),
+                in1=b1_all[:, k_cols].unsqueeze(2).to_broadcast([P, P, PACK]),
+                op=ADD,
+            )
+            u_grouped = stage.tile([P, SIZE], BF16, tag="u_grouped", align_bytes=64)
+            nc.scalar.activation(out=u_grouped[:], in_=biased[:].rearrange("q k t -> q (k t)"), func=GELU)
+            nc.vector.quantize_mx(out=u_codes[:, m, :].bitcast(FP8X4), scales=u_scales[:, m, :], in_=u_grouped[:])
+
+            y = psum.tile([P, SIZE], F32, tag="bank")
+            nc.tensor.matmul_mx(
+                out=y[:],
+                lhsT=u_codes[:, m, :].bitcast(FP8X4),
+                lhsT_scale=u_scales[:, m, :],
+                rhs=w2_codes[:].rearrange("p i r -> p (i r)").bitcast(FP8X4),
+                rhs_scale=w2_scales[:].rearrange("p i r -> p (i r)"),
+                start=True,
+                stop=True,
+            )
+            result = stage.tile([P, SIZE], F32, tag="result")
+            nc.vector.tensor_tensor(out=result[:], in0=y[:], in1=b2_all, op=ADD)
+            nc.sync.dma_start(out=out_rows[k_cols, :], in_=result[:])

@@ -19,19 +19,18 @@ TILES = SIZE // P
 FLOPS = 2 * 2 * SIZE * SIZE * SIZE
 
 
-def quantise_weight_rows(nc, weights, psum, identity, rows, codes, scales):
-    natural = weights.tile([P, SIZE], BF16, tag="natural")
-    nc.sync.dma_start(out=natural[:], in_=rows)
-    words = natural[:].bitcast(F32).rearrange("r (p s) -> r s p", s=2)
+AHEAD = 2
+
+
+def flip_weight_rows(nc, psum, identity, natural, grouped):
+    words = natural.bitcast(F32).rearrange("r (p s) -> r s p", s=2)
     flipped = psum.tile([P, 2, P], F32, tag="bank")
     for s in range(2):
         nc.tensor.transpose(out=flipped[:, s, :], in_=words[:, s, :], identity=identity)
-    grouped = weights.tile([P, SIZE], BF16, tag="grouped", align_bytes=64)
     nc.scalar.copy(
-        out=grouped[:].bitcast(F32).rearrange("p (r s) -> p r s", s=2),
+        out=grouped.bitcast(F32).rearrange("p (r s) -> p r s", s=2),
         in_=flipped[:].rearrange("p s r -> p r s"),
     )
-    nc.vector.quantize_mx(out=codes.bitcast(FP8X4), scales=scales, in_=grouped[:])
 
 
 def tile_getspatialgatingweights_pa_s_kernel(tc, x_norm, w1_u, b1_u, w2, b2, out):
@@ -40,33 +39,39 @@ def tile_getspatialgatingweights_pa_s_kernel(tc, x_norm, w1_u, b1_u, w2, b2, out
     out_rows = out.rearrange("n c d h w -> (n c) (d h w)")
 
     with ExitStack() as ctx:
+        ctx.enter_context(tc.manual_schedule())
         keep = ctx.enter_context(tc.tile_pool(name="keep", bufs=1))
-        weights = ctx.enter_context(tc.tile_pool(name="weights", bufs=2 * TILES))
         stage = ctx.enter_context(tc.tile_pool(name="stage", bufs=TILES))
-        psum_z = ctx.enter_context(tc.psum_pool(name="psum_z", bufs=4))
+        psum_z = ctx.enter_context(tc.psum_pool(name="psum_z", bufs=TILES))
         psum = ctx.enter_context(tc.psum_pool(name="psum", bufs=4))
 
         x_raw = keep.tile([P, PACK, SIZE], BF16)
         nc.sync.dma_start(out=x_raw[:], in_=x_rows.rearrange("(p j) v -> p j v", j=PACK))
-
-        identity = keep.tile([P, P], F32)
-        make_identity(nc, identity[:])
-        ones = keep.tile([P, P], BF16)
-        nc.vector.memset(ones[:], 1.0)
-        zero_column = keep.tile([P, 1], F32)
-        nc.vector.memset(zero_column[:], 0.0)
-        unused_column = keep.tile([P, 1], F32)
-        nc.scalar.activation(out=unused_column[:], in_=zero_column[:], func=GELU)
+        w1_natural = keep.tile([P, TILES, SIZE], BF16)
+        w2_natural = keep.tile([P, TILES, SIZE], BF16)
+        for i in range(TILES):
+            nc.sync.dma_start(out=w1_natural[:, i, :], in_=w1_u[i * P : (i + 1) * P, :])
+        for i in range(TILES):
+            nc.sync.dma_start(out=w2_natural[:, i, :], in_=w2[i * P : (i + 1) * P, :])
 
         bias_rows = keep.tile([P, 2, SIZE], BF16)
         nc.vector.memset(bias_rows[:], 0.0)
         nc.scalar.dma_start(out=bias_rows[0:1, 0, :], in_=b1_u.unsqueeze(0))
         nc.scalar.dma_start(out=bias_rows[0:1, 1, :], in_=b2.unsqueeze(0))
-        bias_all = keep.tile([P, 2, SIZE], F32)
+        ones = keep.tile([P, P], BF16)
+        nc.vector.memset(ones[:], 1.0)
+        identity = keep.tile([P, P], F32)
+        make_identity(nc, identity[:])
+        zero_column = keep.tile([P, 1], F32)
+        nc.vector.memset(zero_column[:], 0.0)
+        unused_column = keep.tile([P, 1], F32)
+        nc.scalar.activation(out=unused_column[:], in_=zero_column[:], func=GELU)
+
+        spread = psum.tile([P, 2, SIZE], BF16, tag="bank")
         for i in range(2):
-            spread = psum.tile([P, SIZE], F32, tag="bank")
-            nc.tensor.matmul(out=spread[:], lhsT=ones[:], rhs=bias_rows[:, i, :], start=True, stop=True)
-            nc.scalar.copy(out=bias_all[:, i, :], in_=spread[:])
+            nc.tensor.matmul(out=spread[:, i, :], lhsT=ones[:], rhs=bias_rows[:, i, :], start=True, stop=True)
+        bias_all = keep.tile([P, 2, SIZE], BF16)
+        nc.scalar.copy(out=bias_all[:], in_=spread[:])
         b1_all = bias_all[:, 0, :]
         b2_all = bias_all[:, 1, :]
 
@@ -79,31 +84,30 @@ def tile_getspatialgatingweights_pa_s_kernel(tc, x_norm, w1_u, b1_u, w2, b2, out
                 nc.vector.tensor_copy(out=x_grouped[:, t], in_=x_sorted[:, t])
             else:
                 nc.scalar.copy(out=x_grouped[:, t], in_=x_sorted[:, t])
-        for t in range(PACK):
-            nc.vector.quantize_mx(
-                out=x_codes[:, t, :].bitcast(FP8X4),
-                scales=x_scales[:, t, :],
-                in_=x_grouped[:, t].rearrange("p q j -> p (q j)"),
-            )
+        nc.vector.quantize_mx(
+            out=x_codes[:].rearrange("p t q -> p (t q)").bitcast(FP8X4),
+            scales=x_scales[:].rearrange("p t q -> p (t q)"),
+            in_=x_grouped[:].rearrange("p t q j -> p (t q j)"),
+        )
 
+        w1_grouped = keep.tile([P, TILES, SIZE], BF16, align_bytes=64)
         w1_codes = keep.tile([P, TILES, P], U32, align_bytes=64)
         w1_scales = keep.tile([P, TILES, P], U8, align_bytes=64)
-        w2_codes = keep.tile([P, TILES, P], U32, align_bytes=64)
-        w2_scales = keep.tile([P, TILES, P], U8, align_bytes=64)
         for i in range(TILES):
-            quantise_weight_rows(
-                nc, weights, psum, identity[:], w1_u[i * P : (i + 1) * P, :], w1_codes[:, i, :], w1_scales[:, i, :]
-            )
-        for i in range(TILES):
-            quantise_weight_rows(
-                nc, weights, psum, identity[:], w2[i * P : (i + 1) * P, :], w2_codes[:, i, :], w2_scales[:, i, :]
+            flip_weight_rows(nc, psum, identity[:], w1_natural[:, i, :], w1_grouped[:, i, :])
+            nc.vector.quantize_mx(
+                out=w1_codes[:, i, :].bitcast(FP8X4), scales=w1_scales[:, i, :], in_=w1_grouped[:, i, :]
             )
 
+        z_banks = []
         u_codes = keep.tile([P, TILES, P], U32, align_bytes=64)
         u_scales = keep.tile([P, TILES, P], U8, align_bytes=64)
-        for m in range(TILES):
-            k_cols = slice(m * P, (m + 1) * P)
-            z = psum_z.tile([P, PACK, P], F32)
+        w2_grouped = keep.tile([P, TILES, SIZE], BF16, align_bytes=64)
+        w2_codes = keep.tile([P, SIZE], U32, align_bytes=64)
+        w2_scales = keep.tile([P, SIZE], U8, align_bytes=64)
+
+        def first_product(m):
+            z = psum_z.tile([P, PACK, P], F32, name="z")
             for t in range(PACK):
                 nc.tensor.matmul_mx(
                     out=z[:, t, :],
@@ -114,27 +118,54 @@ def tile_getspatialgatingweights_pa_s_kernel(tc, x_norm, w1_u, b1_u, w2, b2, out
                     start=True,
                     stop=True,
                 )
+            z_banks.append(z)
+
+        def bias_and_gelu(m):
             biased = stage.tile([P, P, PACK], F32, tag="biased")
             nc.vector.tensor_tensor(
                 out=biased[:],
-                in0=z[:].rearrange("q t k -> q k t"),
-                in1=b1_all[:, k_cols].unsqueeze(2).to_broadcast([P, P, PACK]),
+                in0=z_banks[m][:].rearrange("q t k -> q k t"),
+                in1=b1_all[:, m * P : (m + 1) * P].unsqueeze(2).to_broadcast([P, P, PACK]),
                 op=ADD,
             )
             u_grouped = stage.tile([P, SIZE], BF16, tag="u_grouped", align_bytes=64)
             nc.scalar.activation(out=u_grouped[:], in_=biased[:].rearrange("q k t -> q (k t)"), func=GELU)
-            nc.vector.quantize_mx(out=u_codes[:, m, :].bitcast(FP8X4), scales=u_scales[:, m, :], in_=u_grouped[:])
+            return u_grouped
 
+        def second_product(m, u_grouped):
+            nc.vector.quantize_mx(out=u_codes[:, m, :].bitcast(FP8X4), scales=u_scales[:, m, :], in_=u_grouped[:])
             y = psum.tile([P, SIZE], F32, tag="bank")
             nc.tensor.matmul_mx(
                 out=y[:],
                 lhsT=u_codes[:, m, :].bitcast(FP8X4),
                 lhsT_scale=u_scales[:, m, :],
-                rhs=w2_codes[:].rearrange("p i r -> p (i r)").bitcast(FP8X4),
-                rhs_scale=w2_scales[:].rearrange("p i r -> p (i r)"),
+                rhs=w2_codes[:].bitcast(FP8X4),
+                rhs_scale=w2_scales[:],
                 start=True,
                 stop=True,
             )
+            return y
+
+        def bias_and_store(m, y):
             result = stage.tile([P, SIZE], F32, tag="result")
             nc.vector.tensor_tensor(out=result[:], in0=y[:], in1=b2_all, op=ADD)
-            nc.sync.dma_start(out=out_rows[k_cols, :], in_=result[:])
+            nc.sync.dma_start(out=out_rows[m * P : (m + 1) * P, :], in_=result[:])
+
+        first_product(0)
+        for i in range(TILES):
+            flip_weight_rows(nc, psum, identity[:], w2_natural[:, i, :], w2_grouped[:, i, :])
+        for m in range(1, TILES):
+            first_product(m)
+
+        u_tiles = [bias_and_gelu(m) for m in range(AHEAD)]
+        nc.vector.quantize_mx(
+            out=w2_codes[:].bitcast(FP8X4), scales=w2_scales[:], in_=w2_grouped[:].rearrange("p i c -> p (i c)")
+        )
+        y_banks = []
+        for m in range(TILES):
+            y_banks.append(second_product(m, u_tiles[m]))
+            if m + AHEAD < TILES:
+                u_tiles.append(bias_and_gelu(m + AHEAD))
+            if m >= 1:
+                bias_and_store(m - 1, y_banks[m - 1])
+        bias_and_store(TILES - 1, y_banks[TILES - 1])

@@ -47,17 +47,16 @@ def tile_getspatialgatingweights_pa_s_kernel(tc, x_norm, w1_u, b1_u, w2, b2, out
 
         x_raw = keep.tile([P, PACK, SIZE], BF16)
         nc.sync.dma_start(out=x_raw[:], in_=x_rows.rearrange("(p j) v -> p j v", j=PACK))
+        bias_rows = keep.tile([P, 2, SIZE], BF16)
+        nc.gpsimd.memset(bias_rows[:].bitcast(F32), 0.0)
+        nc.sync.dma_start(out=bias_rows[0:1, 0, :], in_=b1_u.unsqueeze(0))
+        nc.sync.dma_start(out=bias_rows[0:1, 1, :], in_=b2.unsqueeze(0))
         w1_natural = keep.tile([P, TILES, SIZE], BF16)
-        w2_natural = keep.tile([P, TILES, SIZE], BF16)
         for i in range(TILES):
             nc.sync.dma_start(out=w1_natural[:, i, :], in_=w1_u[i * P : (i + 1) * P, :])
-        for i in range(TILES):
-            nc.sync.dma_start(out=w2_natural[:, i, :], in_=w2[i * P : (i + 1) * P, :])
+        w2_natural = keep.tile([P, TILES, SIZE], BF16)
+        nc.sync.dma_start(out=w2_natural[:], in_=w2.rearrange("(i r) g -> r i g", r=P))
 
-        bias_rows = keep.tile([P, 2, SIZE], BF16)
-        nc.vector.memset(bias_rows[:], 0.0)
-        nc.scalar.dma_start(out=bias_rows[0:1, 0, :], in_=b1_u.unsqueeze(0))
-        nc.scalar.dma_start(out=bias_rows[0:1, 1, :], in_=b2.unsqueeze(0))
         ones = keep.tile([P, P], BF16)
         nc.vector.memset(ones[:], 1.0)
         identity = keep.tile([P, P], F32)
@@ -67,13 +66,14 @@ def tile_getspatialgatingweights_pa_s_kernel(tc, x_norm, w1_u, b1_u, w2, b2, out
         unused_column = keep.tile([P, 1], F32)
         nc.scalar.activation(out=unused_column[:], in_=zero_column[:], func=GELU)
 
-        spread = psum.tile([P, 2, SIZE], BF16, tag="bank")
-        for i in range(2):
-            nc.tensor.matmul(out=spread[:, i, :], lhsT=ones[:], rhs=bias_rows[:, i, :], start=True, stop=True)
         bias_all = keep.tile([P, 2, SIZE], BF16)
-        nc.scalar.copy(out=bias_all[:], in_=spread[:])
         b1_all = bias_all[:, 0, :]
         b2_all = bias_all[:, 1, :]
+
+        def spread_bias(i):
+            spread = psum.tile([P, SIZE], BF16, tag="bank")
+            nc.tensor.matmul(out=spread[:], lhsT=ones[:], rhs=bias_rows[:, i, :], start=True, stop=True)
+            nc.scalar.copy(out=bias_all[:, i, :], in_=spread[:])
 
         x_grouped = keep.tile([P, PACK, P, PACK], BF16, align_bytes=64)
         x_codes = keep.tile([P, PACK, P], U32, align_bytes=64)
@@ -90,6 +90,8 @@ def tile_getspatialgatingweights_pa_s_kernel(tc, x_norm, w1_u, b1_u, w2, b2, out
             in_=x_grouped[:].rearrange("p t q j -> p (t q j)"),
         )
 
+        spread_bias(0)
+
         w1_grouped = keep.tile([P, TILES, SIZE], BF16, align_bytes=64)
         w1_codes = keep.tile([P, TILES, P], U32, align_bytes=64)
         w1_scales = keep.tile([P, TILES, P], U8, align_bytes=64)
@@ -100,6 +102,7 @@ def tile_getspatialgatingweights_pa_s_kernel(tc, x_norm, w1_u, b1_u, w2, b2, out
             )
 
         z_banks = []
+        u_tiles = []
         u_codes = keep.tile([P, TILES, P], U32, align_bytes=64)
         u_scales = keep.tile([P, TILES, P], U8, align_bytes=64)
         w2_grouped = keep.tile([P, TILES, SIZE], BF16, align_bytes=64)
@@ -130,10 +133,14 @@ def tile_getspatialgatingweights_pa_s_kernel(tc, x_norm, w1_u, b1_u, w2, b2, out
             )
             u_grouped = stage.tile([P, SIZE], BF16, tag="u_grouped", align_bytes=64)
             nc.scalar.activation(out=u_grouped[:], in_=biased[:].rearrange("q k t -> q (k t)"), func=GELU)
-            return u_grouped
+            u_tiles.append(u_grouped)
 
-        def second_product(m, u_grouped):
-            nc.vector.quantize_mx(out=u_codes[:, m, :].bitcast(FP8X4), scales=u_scales[:, m, :], in_=u_grouped[:])
+        def quantise_u(m):
+            nc.vector.quantize_mx(
+                out=u_codes[:, m, :].bitcast(FP8X4), scales=u_scales[:, m, :], in_=u_tiles[m][:]
+            )
+
+        def second_product(m):
             y = psum.tile([P, SIZE], F32, tag="bank")
             nc.tensor.matmul_mx(
                 out=y[:],
@@ -144,28 +151,25 @@ def tile_getspatialgatingweights_pa_s_kernel(tc, x_norm, w1_u, b1_u, w2, b2, out
                 start=True,
                 stop=True,
             )
-            return y
-
-        def bias_and_store(m, y):
             result = stage.tile([P, SIZE], F32, tag="result")
             nc.vector.tensor_tensor(out=result[:], in0=y[:], in1=b2_all, op=ADD)
             nc.sync.dma_start(out=out_rows[m * P : (m + 1) * P, :], in_=result[:])
 
-        first_product(0)
-        for i in range(TILES):
-            flip_weight_rows(nc, psum, identity[:], w2_natural[:, i, :], w2_grouped[:, i, :])
-        for m in range(1, TILES):
+        spread_bias(1)
+        for m in range(TILES):
             first_product(m)
 
-        u_tiles = [bias_and_gelu(m) for m in range(AHEAD)]
+        for m in range(AHEAD):
+            bias_and_gelu(m)
+        for i in range(TILES):
+            flip_weight_rows(nc, psum, identity[:], w2_natural[:, i, :], w2_grouped[:, i, :])
+        for m in range(AHEAD, TILES):
+            quantise_u(m - AHEAD)
+            bias_and_gelu(m)
         nc.vector.quantize_mx(
             out=w2_codes[:].bitcast(FP8X4), scales=w2_scales[:], in_=w2_grouped[:].rearrange("p i c -> p (i c)")
         )
-        y_banks = []
+        for m in range(TILES - AHEAD, TILES):
+            quantise_u(m)
         for m in range(TILES):
-            y_banks.append(second_product(m, u_tiles[m]))
-            if m + AHEAD < TILES:
-                u_tiles.append(bias_and_gelu(m + AHEAD))
-            if m >= 1:
-                bias_and_store(m - 1, y_banks[m - 1])
-        bias_and_store(TILES - 1, y_banks[TILES - 1])
+            second_product(m)

@@ -13,6 +13,8 @@ GELU = mybir.ActivationFunctionType.Gelu
 
 P = 128
 PACK = 4
+HALVES = 2
+PAIR = 2
 SIZE = P * PACK
 TILES = SIZE // P
 
@@ -23,13 +25,13 @@ AHEAD = 2
 
 
 def flip_weight_rows(nc, psum, identity, natural, grouped):
-    words = natural.bitcast(F32).rearrange("r (p s) -> r s p", s=2)
-    flipped = psum.tile([P, 2, P], F32, tag="bank")
-    for s in range(2):
-        nc.tensor.transpose(out=flipped[:, s, :], in_=words[:, s, :], identity=identity)
+    words = natural.bitcast(F32).rearrange("r (h p) -> r h p", h=HALVES)
+    flipped = psum.tile([P, HALVES, P], F32, tag="bank")
+    for h in range(HALVES):
+        nc.tensor.transpose(out=flipped[:, h, :], in_=words[:, h, :], identity=identity)
     nc.scalar.copy(
-        out=grouped.bitcast(F32).rearrange("p (r s) -> p r s", s=2),
-        in_=flipped[:].rearrange("p s r -> p r s"),
+        out=grouped.bitcast(F32).rearrange("p (r h) -> p r h", h=HALVES),
+        in_=flipped[:].rearrange("p h r -> p r h"),
     )
 
 
@@ -46,7 +48,10 @@ def tile_getspatialgatingweights_pa_s_kernel(tc, x_norm, w1_u, b1_u, w2, b2, out
         psum = ctx.enter_context(tc.psum_pool(name="psum", bufs=4))
 
         x_raw = keep.tile([P, PACK, SIZE], BF16)
-        nc.sync.dma_start(out=x_raw[:], in_=x_rows.rearrange("(p j) v -> p j v", j=PACK))
+        nc.sync.dma_start(
+            out=x_raw[:].rearrange("p (h e) v -> p h e v", h=HALVES),
+            in_=x_rows.rearrange("(h p e) v -> p h e v", h=HALVES, e=PAIR),
+        )
         bias_rows = keep.tile([P, 2, SIZE], BF16)
         nc.gpsimd.memset(bias_rows[:].bitcast(F32), 0.0)
         nc.sync.dma_start(out=bias_rows[0:1, 0, :], in_=b1_u.unsqueeze(0))
@@ -78,12 +83,12 @@ def tile_getspatialgatingweights_pa_s_kernel(tc, x_norm, w1_u, b1_u, w2, b2, out
         x_grouped = keep.tile([P, PACK, P, PACK], BF16, align_bytes=64)
         x_codes = keep.tile([P, PACK, P], U32, align_bytes=64)
         x_scales = keep.tile([P, PACK, P], U8, align_bytes=64)
-        x_sorted = x_raw[:].rearrange("p j (q t) -> p t q j", t=PACK)
+        x_sorted = x_raw[:].rearrange("p j (h q e) -> p h e q j", h=HALVES, e=PAIR)
         for t in range(PACK):
             if t < PACK - 1:
-                nc.vector.tensor_copy(out=x_grouped[:, t], in_=x_sorted[:, t])
+                nc.vector.tensor_copy(out=x_grouped[:, t], in_=x_sorted[:, t // PAIR, t % PAIR])
             else:
-                nc.scalar.copy(out=x_grouped[:, t], in_=x_sorted[:, t])
+                nc.scalar.copy(out=x_grouped[:, t], in_=x_sorted[:, t // PAIR, t % PAIR])
         nc.vector.quantize_mx(
             out=x_codes[:].rearrange("p t q -> p (t q)").bitcast(FP8X4),
             scales=x_scales[:].rearrange("p t q -> p (t q)"),

@@ -89,22 +89,31 @@ def tile_getspatialgatingweights_pa_s_kernel(tc, x_norm, w1_u, b1_u, w2, b2, out
                 nc.vector.tensor_copy(out=x_grouped[:, t], in_=x_sorted[:, t // PAIR, t % PAIR])
             else:
                 nc.scalar.copy(out=x_grouped[:, t], in_=x_sorted[:, t // PAIR, t % PAIR])
-        nc.vector.quantize_mx(
-            out=x_codes[:].rearrange("p t q -> p (t q)").bitcast(FP8X4),
-            scales=x_scales[:].rearrange("p t q -> p (t q)"),
-            in_=x_grouped[:].rearrange("p t q j -> p (t q j)"),
-        )
 
-        spread_bias(0)
+        def quantise_x(t):
+            nc.vector.quantize_mx(
+                out=x_codes[:, t, :].bitcast(FP8X4),
+                scales=x_scales[:, t, :],
+                in_=x_grouped[:, t].rearrange("p q j -> p (q j)"),
+            )
 
         w1_grouped = keep.tile([P, TILES, SIZE], BF16, align_bytes=64)
         w1_codes = keep.tile([P, TILES, P], U32, align_bytes=64)
         w1_scales = keep.tile([P, TILES, P], U8, align_bytes=64)
-        for i in range(TILES):
+
+        def quantise_w1(i):
             flip_weight_rows(nc, psum, identity[:], w1_natural[:, i, :], w1_grouped[:, i, :])
             nc.vector.quantize_mx(
                 out=w1_codes[:, i, :].bitcast(FP8X4), scales=w1_scales[:, i, :], in_=w1_grouped[:, i, :]
             )
+
+        for t in range(PACK - 1):
+            quantise_x(t)
+        spread_bias(0)
+        quantise_w1(0)
+        quantise_x(PACK - 1)
+        for i in range(1, TILES):
+            quantise_w1(i)
 
         z_banks = []
         u_tiles = []
@@ -160,7 +169,6 @@ def tile_getspatialgatingweights_pa_s_kernel(tc, x_norm, w1_u, b1_u, w2, b2, out
             nc.vector.tensor_tensor(out=result[:], in0=y[:], in1=b2_all, op=ADD)
             nc.sync.dma_start(out=out_rows[m * P : (m + 1) * P, :], in_=result[:])
 
-        spread_bias(1)
         for m in range(TILES):
             first_product(m)
 
@@ -168,13 +176,14 @@ def tile_getspatialgatingweights_pa_s_kernel(tc, x_norm, w1_u, b1_u, w2, b2, out
             bias_and_gelu(m)
         for i in range(TILES):
             flip_weight_rows(nc, psum, identity[:], w2_natural[:, i, :], w2_grouped[:, i, :])
+        spread_bias(1)
         for m in range(AHEAD, TILES):
             quantise_u(m - AHEAD)
             bias_and_gelu(m)
         nc.vector.quantize_mx(
             out=w2_codes[:].bitcast(FP8X4), scales=w2_scales[:], in_=w2_grouped[:].rearrange("p i c -> p (i c)")
         )
-        for m in range(TILES - AHEAD, TILES):
-            quantise_u(m)
         for m in range(TILES):
+            if m + AHEAD < TILES:
+                quantise_u(m + AHEAD)
             second_product(m)

@@ -21,20 +21,6 @@ TILES = SIZE // P
 FLOPS = 2 * 2 * SIZE * SIZE * SIZE
 
 
-AHEAD = 2
-
-
-def flip_weight_rows(nc, psum, identity, natural, grouped):
-    words = natural.bitcast(F32).rearrange("r (h p) -> r h p", h=HALVES)
-    flipped = psum.tile([P, HALVES, P], F32, tag="bank")
-    for h in range(HALVES):
-        nc.tensor.transpose(out=flipped[:, h, :], in_=words[:, h, :], identity=identity)
-    nc.scalar.copy(
-        out=grouped.bitcast(F32).rearrange("p (r h) -> p r h", h=HALVES),
-        in_=flipped[:].rearrange("p h r -> p r h"),
-    )
-
-
 def tile_getspatialgatingweights_pa_s_kernel(tc, x_norm, w1_u, b1_u, w2, b2, out):
     nc = tc.nc
     x_rows = x_norm.rearrange("n c d h w -> (n c) (d h w)")
@@ -52,10 +38,12 @@ def tile_getspatialgatingweights_pa_s_kernel(tc, x_norm, w1_u, b1_u, w2, b2, out
             out=x_raw[:].rearrange("p (h e) v -> p h e v", h=HALVES),
             in_=x_rows.rearrange("(h p e) v -> p h e v", h=HALVES, e=PAIR),
         )
-        bias_rows = keep.tile([P, 2, SIZE], BF16)
+        bias_rows = keep.tile([P, P + SIZE], BF16)
+        b1_rows = bias_rows[:, 0:P]
+        b2_rows = bias_rows[:, P : P + SIZE]
         nc.gpsimd.memset(bias_rows[:].bitcast(F32), 0.0)
-        nc.sync.dma_start(out=bias_rows[0:1, 0, :], in_=b1_u.unsqueeze(0))
-        nc.sync.dma_start(out=bias_rows[0:1, 1, :], in_=b2.unsqueeze(0))
+        nc.sync.dma_start(out=bias_rows[0:TILES, 0:P], in_=b1_u.rearrange("(m k) -> m k", k=P))
+        nc.sync.dma_start(out=bias_rows[0:1, P : P + SIZE], in_=b2.unsqueeze(0))
         w1_natural = keep.tile([P, TILES, SIZE], BF16)
         for i in range(TILES):
             nc.sync.dma_start(out=w1_natural[:, i, :], in_=w1_u[i * P : (i + 1) * P, :])
@@ -66,96 +54,87 @@ def tile_getspatialgatingweights_pa_s_kernel(tc, x_norm, w1_u, b1_u, w2, b2, out
         nc.vector.memset(ones[:], 1.0)
         identity = keep.tile([P, P], F32)
         make_identity(nc, identity[:])
+        pick = keep.tile([P, TILES], BF16)
         zero_column = keep.tile([P, 1], F32)
         nc.vector.memset(zero_column[:], 0.0)
         unused_column = keep.tile([P, 1], F32)
         nc.scalar.activation(out=unused_column[:], in_=zero_column[:], func=GELU)
+        nc.vector.tensor_copy(out=pick[:], in_=identity[:, 0:TILES])
 
-        bias_all = keep.tile([P, 2, SIZE], BF16)
-        b1_all = bias_all[:, 0, :]
-        b2_all = bias_all[:, 1, :]
+        b1_turned = psum.tile([P, TILES], F32, tag="bank")
+        nc.tensor.matmul(out=b1_turned[:], lhsT=b1_rows, rhs=pick[:], start=True, stop=True)
+        b1_columns = keep.tile([P, TILES], F32)
 
-        def spread_bias(i):
-            spread = psum.tile([P, SIZE], BF16, tag="bank")
-            nc.tensor.matmul(out=spread[:], lhsT=ones[:], rhs=bias_rows[:, i, :], start=True, stop=True)
-            nc.scalar.copy(out=bias_all[:, i, :], in_=spread[:])
+        x_grouped = keep.tile([P, SIZE, PACK], BF16, align_bytes=64)
+        x_codes = keep.tile([P, SIZE], U32, align_bytes=64)
+        x_scales = keep.tile([P, SIZE], U8, align_bytes=64)
 
-        x_grouped = keep.tile([P, PACK, P, PACK], BF16, align_bytes=64)
-        x_codes = keep.tile([P, PACK, P], U32, align_bytes=64)
-        x_scales = keep.tile([P, PACK, P], U8, align_bytes=64)
-        x_sorted = x_raw[:].rearrange("p j (h q e) -> p h e q j", h=HALVES, e=PAIR)
-        for t in range(PACK):
-            if t < PACK - 1:
-                nc.vector.tensor_copy(out=x_grouped[:, t], in_=x_sorted[:, t // PAIR, t % PAIR])
-            else:
-                nc.scalar.copy(out=x_grouped[:, t], in_=x_sorted[:, t // PAIR, t % PAIR])
+        def group_x(engine_copy, t):
+            columns = slice(t * P, (t + 1) * P)
+            engine_copy(out=x_grouped[:, columns, :], in_=x_raw[:, :, columns].rearrange("p j v -> p v j"))
 
         def quantise_x(t):
+            columns = slice(t * P, (t + 1) * P)
             nc.vector.quantize_mx(
-                out=x_codes[:, t, :].bitcast(FP8X4),
-                scales=x_scales[:, t, :],
-                in_=x_grouped[:, t].rearrange("p q j -> p (q j)"),
+                out=x_codes[:, columns].bitcast(FP8X4),
+                scales=x_scales[:, columns],
+                in_=x_grouped[:, columns, :].rearrange("p v j -> p (v j)"),
+            )
+
+        def flip(natural):
+            words = natural.bitcast(F32).rearrange("r (h p) -> r h p", h=HALVES)
+            flipped = psum.tile([P, HALVES, P], F32, tag="bank")
+            for h in range(HALVES):
+                nc.tensor.transpose(out=flipped[:, h, :], in_=words[:, h, :], identity=identity[:])
+            return flipped
+
+        def fetch(engine_copy, flipped, grouped):
+            engine_copy(
+                out=grouped.bitcast(F32).rearrange("p (r h) -> p r h", h=HALVES),
+                in_=flipped[:].rearrange("p h r -> p r h"),
             )
 
         w1_grouped = keep.tile([P, TILES, SIZE], BF16, align_bytes=64)
         w1_codes = keep.tile([P, TILES, P], U32, align_bytes=64)
         w1_scales = keep.tile([P, TILES, P], U8, align_bytes=64)
+        w2_grouped = keep.tile([P, TILES, SIZE], BF16, align_bytes=64)
+        w2_codes = keep.tile([P, SIZE], U32, align_bytes=64)
+        w2_scales = keep.tile([P, SIZE], U8, align_bytes=64)
+        u_grouped = keep.tile([P, TILES, SIZE], BF16, align_bytes=64)
+        u_codes = keep.tile([P, TILES, P], U32, align_bytes=64)
+        u_scales = keep.tile([P, TILES, P], U8, align_bytes=64)
+        b2_all = keep.tile([P, SIZE], BF16)
 
         def quantise_w1(i):
-            flip_weight_rows(nc, psum, identity[:], w1_natural[:, i, :], w1_grouped[:, i, :])
             nc.vector.quantize_mx(
                 out=w1_codes[:, i, :].bitcast(FP8X4), scales=w1_scales[:, i, :], in_=w1_grouped[:, i, :]
             )
 
-        for t in range(PACK - 1):
-            quantise_x(t)
-        spread_bias(0)
-        quantise_w1(0)
-        quantise_x(PACK - 1)
-        for i in range(1, TILES):
-            quantise_w1(i)
-
-        z_banks = []
-        u_tiles = []
-        u_codes = keep.tile([P, TILES, P], U32, align_bytes=64)
-        u_scales = keep.tile([P, TILES, P], U8, align_bytes=64)
-        w2_grouped = keep.tile([P, TILES, SIZE], BF16, align_bytes=64)
-        w2_codes = keep.tile([P, SIZE], U32, align_bytes=64)
-        w2_scales = keep.tile([P, SIZE], U8, align_bytes=64)
-
-        def first_product(m):
-            z = psum_z.tile([P, PACK, P], F32, name="z")
-            for t in range(PACK):
-                nc.tensor.matmul_mx(
-                    out=z[:, t, :],
-                    lhsT=x_codes[:, t, :].bitcast(FP8X4),
-                    lhsT_scale=x_scales[:, t, :],
-                    rhs=w1_codes[:, m, :].bitcast(FP8X4),
-                    rhs_scale=w1_scales[:, m, :],
-                    start=True,
-                    stop=True,
-                )
-            z_banks.append(z)
-
-        def bias_and_gelu(m):
-            biased = stage.tile([P, P, PACK], F32, tag="biased")
-            nc.vector.tensor_tensor(
-                out=biased[:],
-                in0=z_banks[m][:].rearrange("q t k -> q k t"),
-                in1=b1_all[:, m * P : (m + 1) * P].unsqueeze(2).to_broadcast([P, P, PACK]),
-                op=ADD,
-            )
-            u_grouped = stage.tile([P, SIZE], BF16, tag="u_grouped", align_bytes=64)
-            nc.scalar.activation(out=u_grouped[:], in_=biased[:].rearrange("q k t -> q (k t)"), func=GELU)
-            u_tiles.append(u_grouped)
-
         def quantise_u(m):
             nc.vector.quantize_mx(
-                out=u_codes[:, m, :].bitcast(FP8X4), scales=u_scales[:, m, :], in_=u_tiles[m][:]
+                out=u_codes[:, m, :].bitcast(FP8X4), scales=u_scales[:, m, :], in_=u_grouped[:, m, :]
             )
 
+        def first_product(m):
+            z = psum_z.tile([P, SIZE], F32, tag="product")
+            nc.tensor.matmul_mx(
+                out=z[:],
+                lhsT=w1_codes[:, m, :].bitcast(FP8X4),
+                lhsT_scale=w1_scales[:, m, :],
+                rhs=x_codes[:].bitcast(FP8X4),
+                rhs_scale=x_scales[:],
+                start=True,
+                stop=True,
+            )
+            return z
+
+        def gelu(m, z):
+            u = stage.tile([P, SIZE], BF16, tag="u")
+            nc.scalar.activation(out=u[:], in_=z[:], func=GELU, bias=b1_columns[:, m : m + 1])
+            return u
+
         def second_product(m):
-            y = psum.tile([P, SIZE], F32, tag="bank")
+            y = psum_z.tile([P, SIZE], F32, tag="product")
             nc.tensor.matmul_mx(
                 out=y[:],
                 lhsT=u_codes[:, m, :].bitcast(FP8X4),
@@ -165,25 +144,58 @@ def tile_getspatialgatingweights_pa_s_kernel(tc, x_norm, w1_u, b1_u, w2, b2, out
                 start=True,
                 stop=True,
             )
+            return y
+
+        def add_b2_and_store(m, y, pieces):
             result = stage.tile([P, SIZE], F32, tag="result")
-            nc.vector.tensor_tensor(out=result[:], in0=y[:], in1=b2_all, op=ADD)
-            nc.sync.dma_start(out=out_rows[m * P : (m + 1) * P, :], in_=result[:])
+            width = SIZE // pieces
+            for i in range(pieces):
+                columns = slice(i * width, (i + 1) * width)
+                nc.vector.tensor_tensor(out=result[:, columns], in0=y[:, columns], in1=b2_all[:, columns], op=ADD)
+                nc.sync.dma_start(out=out_rows[m * P : (m + 1) * P, columns], in_=result[:, columns])
 
-        for m in range(TILES):
-            first_product(m)
-
-        for m in range(AHEAD):
-            bias_and_gelu(m)
+        for t in range(PACK - 1):
+            group_x(nc.vector.tensor_copy, t)
+        group_x(nc.scalar.copy, PACK - 1)
+        nc.vector.tensor_copy(out=b1_columns[:], in_=b1_turned[:])
+        w1_flipped = [flip(w1_natural[:, i, :]) for i in range(TILES)]
         for i in range(TILES):
-            flip_weight_rows(nc, psum, identity[:], w2_natural[:, i, :], w2_grouped[:, i, :])
-        spread_bias(1)
-        for m in range(AHEAD, TILES):
-            quantise_u(m - AHEAD)
-            bias_and_gelu(m)
+            fetch(nc.scalar.copy, w1_flipped[i], w1_grouped[:, i, :])
+        for t in range(PACK - 1):
+            quantise_x(t)
+        quantise_w1(0)
+        quantise_x(PACK - 1)
+        for i in range(1, TILES):
+            quantise_w1(i)
+
+        z = [first_product(m) for m in range(TILES)]
+        u = [gelu(m, z[m]) for m in range(TILES)]
+
+        for i in range(TILES):
+            fetch(nc.vector.tensor_copy, flip(w2_natural[:, i, :]), w2_grouped[:, i, :])
+
+        u_flipped = [flip(u[m][:]) for m in range(2)]
+        fetch(nc.vector.tensor_copy, u_flipped[0], u_grouped[:, 0, :])
         nc.vector.quantize_mx(
             out=w2_codes[:].bitcast(FP8X4), scales=w2_scales[:], in_=w2_grouped[:].rearrange("p i c -> p (i c)")
         )
-        for m in range(TILES):
-            if m + AHEAD < TILES:
-                quantise_u(m + AHEAD)
-            second_product(m)
+        quantise_u(0)
+        fetch(nc.vector.tensor_copy, u_flipped[1], u_grouped[:, 1, :])
+        b2_spread = psum.tile([P, SIZE], BF16, tag="bank")
+        nc.tensor.matmul(out=b2_spread[:], lhsT=ones[:], rhs=b2_rows, start=True, stop=True)
+        nc.scalar.copy(out=b2_all[:], in_=b2_spread[:])
+        y0 = second_product(0)
+        u_flipped.append(flip(u[2][:]))
+        fetch(nc.scalar.copy, u_flipped[2], u_grouped[:, 2, :])
+        quantise_u(1)
+        y1 = second_product(1)
+        u_flipped.append(flip(u[3][:]))
+        fetch(nc.scalar.copy, u_flipped[3], u_grouped[:, 3, :])
+        add_b2_and_store(0, y0, 1)
+        quantise_u(2)
+        y2 = second_product(2)
+        add_b2_and_store(1, y1, 1)
+        quantise_u(3)
+        y3 = second_product(3)
+        add_b2_and_store(2, y2, 1)
+        add_b2_and_store(3, y3, 2)

@@ -24,7 +24,7 @@ FLOPS = 2 * 2 * SIZE * SIZE * SIZE
 def tile_getspatialgatingweights_pa_s_kernel(tc, x_norm, w1_u, b1_u, w2, b2, out):
     nc = tc.nc
     x_rows = x_norm.rearrange("n c d h w -> (n c) (d h w)")
-    out_rows = out.rearrange("n c d h w -> (n c) (d h w)")
+    out_rows = out.rearrange("n (k m) d h w -> m (n k) (d h w)", m=TILES)
 
     with ExitStack() as ctx:
         ctx.enter_context(tc.manual_schedule())
@@ -38,32 +38,31 @@ def tile_getspatialgatingweights_pa_s_kernel(tc, x_norm, w1_u, b1_u, w2, b2, out
             out=x_raw[:].rearrange("p (h e) v -> p h e v", h=HALVES),
             in_=x_rows.rearrange("(h p e) v -> p h e v", h=HALVES, e=PAIR),
         )
-        bias_rows = keep.tile([P, P + SIZE], BF16)
-        b1_rows = bias_rows[:, 0:P]
-        b2_rows = bias_rows[:, P : P + SIZE]
-        nc.gpsimd.memset(bias_rows[:].bitcast(F32), 0.0)
-        nc.sync.dma_start(out=bias_rows[0:TILES, 0:P], in_=b1_u.rearrange("(m k) -> m k", k=P))
-        nc.sync.dma_start(out=bias_rows[0:1, P : P + SIZE], in_=b2.unsqueeze(0))
+        w1_rows = w1_u.rearrange("(r i) c -> r i c", i=TILES)
         w1_natural = keep.tile([P, TILES, SIZE], BF16)
-        for i in range(TILES):
-            nc.sync.dma_start(out=w1_natural[:, i, :], in_=w1_u[i * P : (i + 1) * P, :])
+        nc.sync.dma_start(out=w1_natural[:, 0:2, :], in_=w1_rows[:, 0:2, :])
+        b1_columns = keep.tile([P, TILES], BF16)
+        nc.sync.dma_start(out=b1_columns[:], in_=b1_u.rearrange("(k m) -> k m", m=TILES))
+        b2_rows = keep.tile([P, SIZE], BF16)
+        nc.gpsimd.memset(b2_rows[:].bitcast(F32), 0.0)
+        nc.sync.dma_start(out=b2_rows[0:1, :], in_=b2.unsqueeze(0))
+        nc.sync.dma_start(out=w1_natural[:, 2:4, :], in_=w1_rows[:, 2:4, :])
         w2_natural = keep.tile([P, TILES, SIZE], BF16)
-        nc.sync.dma_start(out=w2_natural[:], in_=w2.rearrange("(i r) g -> r i g", r=P))
+        nc.sync.dma_start(out=w2_natural[:], in_=w2.rearrange("(r i) g -> r i g", i=TILES))
 
+        constant = keep.tile([P, P], F32)
+        nc.vector.memset(constant[:], 0.0)
+        unread = psum.tile([P, P], F32, tag="bank")
+        for n in range(5):
+            nc.tensor.matmul(out=unread[:], lhsT=constant[:], rhs=constant[:], start=True, stop=True)
         ones = keep.tile([P, P], BF16)
         nc.vector.memset(ones[:], 1.0)
         identity = keep.tile([P, P], F32)
         make_identity(nc, identity[:])
-        pick = keep.tile([P, TILES], BF16)
         zero_column = keep.tile([P, 1], F32)
         nc.vector.memset(zero_column[:], 0.0)
         unused_column = keep.tile([P, 1], F32)
         nc.scalar.activation(out=unused_column[:], in_=zero_column[:], func=GELU)
-        nc.vector.tensor_copy(out=pick[:], in_=identity[:, 0:TILES])
-
-        b1_turned = psum.tile([P, TILES], F32, tag="bank")
-        nc.tensor.matmul(out=b1_turned[:], lhsT=b1_rows, rhs=pick[:], start=True, stop=True)
-        b1_columns = keep.tile([P, TILES], F32)
 
         x_grouped = keep.tile([P, SIZE, PACK], BF16, align_bytes=64)
         x_codes = keep.tile([P, SIZE], U32, align_bytes=64)
@@ -98,22 +97,25 @@ def tile_getspatialgatingweights_pa_s_kernel(tc, x_norm, w1_u, b1_u, w2, b2, out
         w1_codes = keep.tile([P, TILES, P], U32, align_bytes=64)
         w1_scales = keep.tile([P, TILES, P], U8, align_bytes=64)
         w2_grouped = keep.tile([P, TILES, SIZE], BF16, align_bytes=64)
-        w2_codes = keep.tile([P, SIZE], U32, align_bytes=64)
-        w2_scales = keep.tile([P, SIZE], U8, align_bytes=64)
+        w2_codes = keep.tile([P, TILES, P], U32, align_bytes=64)
+        w2_scales = keep.tile([P, TILES, P], U8, align_bytes=64)
         u_grouped = keep.tile([P, TILES, SIZE], BF16, align_bytes=64)
         u_codes = keep.tile([P, TILES, P], U32, align_bytes=64)
         u_scales = keep.tile([P, TILES, P], U8, align_bytes=64)
         b2_all = keep.tile([P, SIZE], BF16)
 
-        def quantise_w1(i):
+        def quantise(codes, scales, grouped, tiles):
             nc.vector.quantize_mx(
-                out=w1_codes[:, i, :].bitcast(FP8X4), scales=w1_scales[:, i, :], in_=w1_grouped[:, i, :]
+                out=codes[:, tiles, :].rearrange("p i r -> p (i r)").bitcast(FP8X4),
+                scales=scales[:, tiles, :].rearrange("p i r -> p (i r)"),
+                in_=grouped[:, tiles, :].rearrange("p i c -> p (i c)"),
             )
 
+        def quantise_w1(i):
+            quantise(w1_codes, w1_scales, w1_grouped, slice(i, i + 1))
+
         def quantise_u(m):
-            nc.vector.quantize_mx(
-                out=u_codes[:, m, :].bitcast(FP8X4), scales=u_scales[:, m, :], in_=u_grouped[:, m, :]
-            )
+            quantise(u_codes, u_scales, u_grouped, slice(m, m + 1))
 
         def first_product(m):
             z = psum_z.tile([P, SIZE], F32, tag="product")
@@ -139,8 +141,8 @@ def tile_getspatialgatingweights_pa_s_kernel(tc, x_norm, w1_u, b1_u, w2, b2, out
                 out=y[:],
                 lhsT=u_codes[:, m, :].bitcast(FP8X4),
                 lhsT_scale=u_scales[:, m, :],
-                rhs=w2_codes[:].bitcast(FP8X4),
-                rhs_scale=w2_scales[:],
+                rhs=w2_codes[:].rearrange("p i r -> p (i r)").bitcast(FP8X4),
+                rhs_scale=w2_scales[:].rearrange("p i r -> p (i r)"),
                 start=True,
                 stop=True,
             )
@@ -148,19 +150,27 @@ def tile_getspatialgatingweights_pa_s_kernel(tc, x_norm, w1_u, b1_u, w2, b2, out
 
         def add_b2_and_store(m, y, pieces):
             result = stage.tile([P, SIZE], F32, tag="result")
-            width = SIZE // pieces
-            for i in range(pieces):
-                columns = slice(i * width, (i + 1) * width)
-                nc.vector.tensor_tensor(out=result[:, columns], in0=y[:, columns], in1=b2_all[:, columns], op=ADD)
-                nc.sync.dma_start(out=out_rows[m * P : (m + 1) * P, columns], in_=result[:, columns])
+            y_sorted = y[:].rearrange("k (i r) -> k r i", i=TILES)
+            width = P // pieces
+            for n in range(pieces):
+                r = slice(n * width, (n + 1) * width)
+                cells = slice(n * width * TILES, (n + 1) * width * TILES)
+                nc.vector.tensor_tensor(
+                    out=result[:, cells].rearrange("k (r i) -> k r i", i=TILES),
+                    in0=y_sorted[:, r, :],
+                    in1=b2_all[:, cells].rearrange("k (r i) -> k r i", i=TILES),
+                    op=ADD,
+                )
+                nc.sync.dma_start(out=out_rows[m][:, cells], in_=result[:, cells])
 
         for t in range(PACK - 1):
             group_x(nc.vector.tensor_copy, t)
         group_x(nc.scalar.copy, PACK - 1)
-        nc.vector.tensor_copy(out=b1_columns[:], in_=b1_turned[:])
-        w1_flipped = [flip(w1_natural[:, i, :]) for i in range(TILES)]
         for i in range(TILES):
-            fetch(nc.scalar.copy, w1_flipped[i], w1_grouped[:, i, :])
+            fetch(nc.scalar.copy, flip(w1_natural[:, i, :]), w1_grouped[:, i, :])
+        b2_spread = psum.tile([P, SIZE], BF16, tag="bank")
+        nc.tensor.matmul(out=b2_spread[:], lhsT=ones[:], rhs=b2_rows[:], start=True, stop=True)
+        nc.scalar.copy(out=b2_all[:], in_=b2_spread[:])
         for t in range(PACK - 1):
             quantise_x(t)
         quantise_w1(0)
@@ -168,29 +178,33 @@ def tile_getspatialgatingweights_pa_s_kernel(tc, x_norm, w1_u, b1_u, w2, b2, out
         for i in range(1, TILES):
             quantise_w1(i)
 
-        z = [first_product(m) for m in range(TILES)]
-        u = [gelu(m, z[m]) for m in range(TILES)]
+        z0 = first_product(0)
+        z1 = first_product(1)
+        w2_flipped = [flip(w2_natural[:, i, :]) for i in range(TILES)]
+        u0 = gelu(0, z0)
+        u0_flipped = flip(u0[:])
+        z2 = first_product(2)
+        z3 = first_product(3)
+        fetch(nc.vector.tensor_copy, w2_flipped[0], w2_grouped[:, 0, :])
+        fetch(nc.vector.tensor_copy, w2_flipped[1], w2_grouped[:, 1, :])
+        fetch(nc.scalar.copy, w2_flipped[2], w2_grouped[:, 2, :])
+        fetch(nc.scalar.copy, w2_flipped[3], w2_grouped[:, 3, :])
+        u1 = gelu(1, z1)
+        u2 = gelu(2, z2)
+        u3 = gelu(3, z3)
 
-        for i in range(TILES):
-            fetch(nc.vector.tensor_copy, flip(w2_natural[:, i, :]), w2_grouped[:, i, :])
-
-        u_flipped = [flip(u[m][:]) for m in range(2)]
-        fetch(nc.vector.tensor_copy, u_flipped[0], u_grouped[:, 0, :])
-        nc.vector.quantize_mx(
-            out=w2_codes[:].bitcast(FP8X4), scales=w2_scales[:], in_=w2_grouped[:].rearrange("p i c -> p (i c)")
-        )
+        fetch(nc.vector.tensor_copy, u0_flipped, u_grouped[:, 0, :])
+        quantise(w2_codes, w2_scales, w2_grouped, slice(0, TILES))
         quantise_u(0)
-        fetch(nc.vector.tensor_copy, u_flipped[1], u_grouped[:, 1, :])
-        b2_spread = psum.tile([P, SIZE], BF16, tag="bank")
-        nc.tensor.matmul(out=b2_spread[:], lhsT=ones[:], rhs=b2_rows, start=True, stop=True)
-        nc.scalar.copy(out=b2_all[:], in_=b2_spread[:])
+        u1_flipped = flip(u1[:])
+        u2_flipped = flip(u2[:])
         y0 = second_product(0)
-        u_flipped.append(flip(u[2][:]))
-        fetch(nc.scalar.copy, u_flipped[2], u_grouped[:, 2, :])
+        u3_flipped = flip(u3[:])
+        fetch(nc.vector.tensor_copy, u1_flipped, u_grouped[:, 1, :])
+        fetch(nc.scalar.copy, u2_flipped, u_grouped[:, 2, :])
+        fetch(nc.scalar.copy, u3_flipped, u_grouped[:, 3, :])
         quantise_u(1)
         y1 = second_product(1)
-        u_flipped.append(flip(u[3][:]))
-        fetch(nc.scalar.copy, u_flipped[3], u_grouped[:, 3, :])
         add_b2_and_store(0, y0, 1)
         quantise_u(2)
         y2 = second_product(2)

@@ -30,8 +30,9 @@ def tile_getspatialgatingweights_pa_s_kernel(tc, x_norm, w1_u, b1_u, w2, b2, out
         ctx.enter_context(tc.manual_schedule())
         keep = ctx.enter_context(tc.tile_pool(name="keep", bufs=1))
         stage = ctx.enter_context(tc.tile_pool(name="stage", bufs=TILES))
-        psum_z = ctx.enter_context(tc.psum_pool(name="psum_z", bufs=TILES))
-        psum = ctx.enter_context(tc.psum_pool(name="psum", bufs=4))
+        psum = ctx.enter_context(tc.psum_pool(name="psum", bufs=1))
+        weight_banks = ["weight%d" % i for i in range(TILES)]
+        chunk_banks = ["chunk%d" % m for m in range(TILES)]
 
         x_raw = keep.tile([P, PACK, SIZE], BF16)
         nc.sync.dma_start(
@@ -40,19 +41,20 @@ def tile_getspatialgatingweights_pa_s_kernel(tc, x_norm, w1_u, b1_u, w2, b2, out
         )
         w1_rows = w1_u.rearrange("(r i) c -> r i c", i=TILES)
         w1_natural = keep.tile([P, TILES, SIZE], BF16)
-        nc.sync.dma_start(out=w1_natural[:, 0:2, :], in_=w1_rows[:, 0:2, :])
+        nc.sync.dma_start(out=w1_natural[:, 0, :], in_=w1_rows[:, 0, :])
         b1_columns = keep.tile([P, TILES], BF16)
         nc.sync.dma_start(out=b1_columns[:], in_=b1_u.rearrange("(k m) -> k m", m=TILES))
         b2_rows = keep.tile([P, SIZE], BF16)
         nc.gpsimd.memset(b2_rows[:].bitcast(F32), 0.0)
         nc.sync.dma_start(out=b2_rows[0:1, :], in_=b2.unsqueeze(0))
+        nc.sync.dma_start(out=w1_natural[:, 1, :], in_=w1_rows[:, 1, :])
         nc.sync.dma_start(out=w1_natural[:, 2:4, :], in_=w1_rows[:, 2:4, :])
         w2_natural = keep.tile([P, TILES, SIZE], BF16)
         nc.sync.dma_start(out=w2_natural[:], in_=w2.rearrange("(r i) g -> r i g", i=TILES))
 
         constant = keep.tile([P, P], F32)
         nc.vector.memset(constant[:], 0.0)
-        unread = psum.tile([P, P], F32, tag="bank")
+        unread = psum.tile([P, P], F32, tag=weight_banks[3])
         for n in range(5):
             nc.tensor.matmul(out=unread[:], lhsT=constant[:], rhs=constant[:], start=True, stop=True)
         ones = keep.tile([P, P], BF16)
@@ -80,9 +82,9 @@ def tile_getspatialgatingweights_pa_s_kernel(tc, x_norm, w1_u, b1_u, w2, b2, out
                 in_=x_grouped[:, columns, :].rearrange("p v j -> p (v j)"),
             )
 
-        def flip(natural):
+        def flip(natural, bank):
             words = natural.bitcast(F32).rearrange("r (h p) -> r h p", h=HALVES)
-            flipped = psum.tile([P, HALVES, P], F32, tag="bank")
+            flipped = psum.tile([P, HALVES, P], F32, tag=bank)
             for h in range(HALVES):
                 nc.tensor.transpose(out=flipped[:, h, :], in_=words[:, h, :], identity=identity[:])
             return flipped
@@ -117,26 +119,32 @@ def tile_getspatialgatingweights_pa_s_kernel(tc, x_norm, w1_u, b1_u, w2, b2, out
         def quantise_u(m):
             quantise(u_codes, u_scales, u_grouped, slice(m, m + 1))
 
-        def first_product(m):
-            z = psum_z.tile([P, SIZE], F32, tag="product")
-            nc.tensor.matmul_mx(
-                out=z[:],
-                lhsT=w1_codes[:, m, :].bitcast(FP8X4),
-                lhsT_scale=w1_scales[:, m, :],
-                rhs=x_codes[:].bitcast(FP8X4),
-                rhs_scale=x_scales[:],
-                start=True,
-                stop=True,
-            )
+        def first_product(m, pieces):
+            z = psum.tile([P, SIZE], F32, tag=chunk_banks[m])
+            width = SIZE // pieces
+            for n in range(pieces):
+                cells = slice(n * width, (n + 1) * width)
+                nc.tensor.matmul_mx(
+                    out=z[:, cells],
+                    lhsT=w1_codes[:, m, :].bitcast(FP8X4),
+                    lhsT_scale=w1_scales[:, m, :],
+                    rhs=x_codes[:, cells].bitcast(FP8X4),
+                    rhs_scale=x_scales[:, cells],
+                    start=True,
+                    stop=True,
+                )
             return z
 
-        def gelu(m, z):
+        def gelu(m, z, pieces):
             u = stage.tile([P, SIZE], BF16, tag="u")
-            nc.scalar.activation(out=u[:], in_=z[:], func=GELU, bias=b1_columns[:, m : m + 1])
+            width = SIZE // pieces
+            for n in range(pieces):
+                cells = slice(n * width, (n + 1) * width)
+                nc.scalar.activation(out=u[:, cells], in_=z[:, cells], func=GELU, bias=b1_columns[:, m : m + 1])
             return u
 
         def second_product(m):
-            y = psum_z.tile([P, SIZE], F32, tag="product")
+            y = psum.tile([P, SIZE], F32, tag=chunk_banks[m])
             nc.tensor.matmul_mx(
                 out=y[:],
                 lhsT=u_codes[:, m, :].bitcast(FP8X4),
@@ -166,42 +174,47 @@ def tile_getspatialgatingweights_pa_s_kernel(tc, x_norm, w1_u, b1_u, w2, b2, out
         for t in range(PACK - 1):
             group_x(nc.vector.tensor_copy, t)
         group_x(nc.scalar.copy, PACK - 1)
-        for i in range(TILES):
-            fetch(nc.scalar.copy, flip(w1_natural[:, i, :]), w1_grouped[:, i, :])
-        b2_spread = psum.tile([P, SIZE], BF16, tag="bank")
+        w1_flipped = [flip(w1_natural[:, i, :], weight_banks[i]) for i in range(2)]
+        b2_spread = psum.tile([P, SIZE], BF16, tag=chunk_banks[3])
         nc.tensor.matmul(out=b2_spread[:], lhsT=ones[:], rhs=b2_rows[:], start=True, stop=True)
+        w1_flipped.extend([flip(w1_natural[:, i, :], weight_banks[i]) for i in range(2, TILES)])
+        fetch(nc.scalar.copy, w1_flipped[0], w1_grouped[:, 0, :])
+        fetch(nc.scalar.copy, w1_flipped[1], w1_grouped[:, 1, :])
         nc.scalar.copy(out=b2_all[:], in_=b2_spread[:])
         for t in range(PACK - 1):
             quantise_x(t)
         quantise_w1(0)
         quantise_x(PACK - 1)
-        for i in range(1, TILES):
-            quantise_w1(i)
+        quantise_w1(1)
+        fetch(nc.vector.tensor_copy, w1_flipped[2], w1_grouped[:, 2, :])
+        fetch(nc.vector.tensor_copy, w1_flipped[3], w1_grouped[:, 3, :])
+        quantise_w1(2)
+        quantise_w1(3)
 
-        z0 = first_product(0)
-        z1 = first_product(1)
-        w2_flipped = [flip(w2_natural[:, i, :]) for i in range(TILES)]
-        u0 = gelu(0, z0)
-        u0_flipped = flip(u0[:])
-        z2 = first_product(2)
-        z3 = first_product(3)
+        z0 = first_product(0, 2)
+        z1 = first_product(1, 1)
+        w2_flipped = [flip(w2_natural[:, i, :], weight_banks[i]) for i in range(TILES)]
+        u0 = gelu(0, z0, 2)
+        u0_flipped = flip(u0[:], chunk_banks[0])
+        z2 = first_product(2, 1)
+        z3 = first_product(3, 1)
         fetch(nc.vector.tensor_copy, w2_flipped[0], w2_grouped[:, 0, :])
         fetch(nc.vector.tensor_copy, w2_flipped[1], w2_grouped[:, 1, :])
         fetch(nc.scalar.copy, w2_flipped[2], w2_grouped[:, 2, :])
         fetch(nc.scalar.copy, w2_flipped[3], w2_grouped[:, 3, :])
-        u1 = gelu(1, z1)
-        u2 = gelu(2, z2)
-        u3 = gelu(3, z3)
+        u1 = gelu(1, z1, 1)
+        u2 = gelu(2, z2, 1)
+        u3 = gelu(3, z3, 1)
 
         fetch(nc.vector.tensor_copy, u0_flipped, u_grouped[:, 0, :])
         quantise(w2_codes, w2_scales, w2_grouped, slice(0, TILES))
         quantise_u(0)
-        u1_flipped = flip(u1[:])
-        u2_flipped = flip(u2[:])
-        y0 = second_product(0)
-        u3_flipped = flip(u3[:])
+        u1_flipped = flip(u1[:], chunk_banks[1])
         fetch(nc.vector.tensor_copy, u1_flipped, u_grouped[:, 1, :])
+        u2_flipped = flip(u2[:], chunk_banks[2])
         fetch(nc.scalar.copy, u2_flipped, u_grouped[:, 2, :])
+        y0 = second_product(0)
+        u3_flipped = flip(u3[:], chunk_banks[3])
         fetch(nc.scalar.copy, u3_flipped, u_grouped[:, 3, :])
         quantise_u(1)
         y1 = second_product(1)

@@ -54,9 +54,13 @@ def tile_getspatialgatingweights_pa_s_kernel(tc, x_norm, w1_u, b1_u, w2, b2, out
 
         constant = keep.tile([P, P], F32)
         nc.vector.memset(constant[:], 0.0)
-        unread = psum.tile([P, P], F32, tag=weight_banks[3])
-        for n in range(5):
-            nc.tensor.matmul(out=unread[:], lhsT=constant[:], rhs=constant[:], start=True, stop=True)
+        unread = psum.tile([P, P], F32, tag=chunk_banks[3])
+
+        def keep_clock(count):
+            for n in range(count):
+                nc.tensor.matmul(out=unread[:], lhsT=constant[:], rhs=constant[:], start=True, stop=True)
+
+        keep_clock(4)
         ones = keep.tile([P, P], BF16)
         nc.vector.memset(ones[:], 1.0)
         identity = keep.tile([P, P], F32)
@@ -70,12 +74,10 @@ def tile_getspatialgatingweights_pa_s_kernel(tc, x_norm, w1_u, b1_u, w2, b2, out
         x_codes = keep.tile([P, SIZE], U32, align_bytes=64)
         x_scales = keep.tile([P, SIZE], U8, align_bytes=64)
 
-        def group_x(engine_copy, t):
-            columns = slice(t * P, (t + 1) * P)
+        def group_x(engine_copy, columns):
             engine_copy(out=x_grouped[:, columns, :], in_=x_raw[:, :, columns].rearrange("p j v -> p v j"))
 
-        def quantise_x(t):
-            columns = slice(t * P, (t + 1) * P)
+        def quantise_x(columns):
             nc.vector.quantize_mx(
                 out=x_codes[:, columns].bitcast(FP8X4),
                 scales=x_scales[:, columns],
@@ -83,16 +85,18 @@ def tile_getspatialgatingweights_pa_s_kernel(tc, x_norm, w1_u, b1_u, w2, b2, out
             )
 
         def flip(natural, bank):
-            words = natural.bitcast(F32).rearrange("r (h p) -> r h p", h=HALVES)
-            flipped = psum.tile([P, HALVES, P], F32, tag=bank)
-            for h in range(HALVES):
-                nc.tensor.transpose(out=flipped[:, h, :], in_=words[:, h, :], identity=identity[:])
+            tiles = len(natural)
+            flipped = psum.tile([P, tiles, HALVES, P], F32, tag=bank)
+            for i in range(tiles):
+                words = natural[i].bitcast(F32).rearrange("r (h p) -> r h p", h=HALVES)
+                for h in range(HALVES):
+                    nc.tensor.transpose(out=flipped[:, i, h, :], in_=words[:, h, :], identity=identity[:])
             return flipped
 
         def fetch(engine_copy, flipped, grouped):
             engine_copy(
-                out=grouped.bitcast(F32).rearrange("p (r h) -> p r h", h=HALVES),
-                in_=flipped[:].rearrange("p h r -> p r h"),
+                out=grouped.rearrange("p i c -> p (i c)").bitcast(F32).rearrange("p (i r h) -> p i r h", r=P, h=HALVES),
+                in_=flipped[:].rearrange("p i h r -> p i r h"),
             )
 
         w1_grouped = keep.tile([P, TILES, SIZE], BF16, align_bytes=64)
@@ -113,8 +117,8 @@ def tile_getspatialgatingweights_pa_s_kernel(tc, x_norm, w1_u, b1_u, w2, b2, out
                 in_=grouped[:, tiles, :].rearrange("p i c -> p (i c)"),
             )
 
-        def quantise_w1(i):
-            quantise(w1_codes, w1_scales, w1_grouped, slice(i, i + 1))
+        def quantise_w1(tiles):
+            quantise(w1_codes, w1_scales, w1_grouped, tiles)
 
         def quantise_u(m):
             quantise(u_codes, u_scales, u_grouped, slice(m, m + 1))
@@ -171,52 +175,53 @@ def tile_getspatialgatingweights_pa_s_kernel(tc, x_norm, w1_u, b1_u, w2, b2, out
                 )
                 nc.sync.dma_start(out=out_rows[m][:, cells], in_=result[:, cells])
 
-        for t in range(PACK - 1):
-            group_x(nc.vector.tensor_copy, t)
-        group_x(nc.scalar.copy, PACK - 1)
-        w1_flipped = [flip(w1_natural[:, i, :], weight_banks[i]) for i in range(2)]
-        b2_spread = psum.tile([P, SIZE], BF16, tag=chunk_banks[3])
+        half = SIZE // 2
+        share = SIZE * 5 // 8
+        group_x(nc.vector.tensor_copy, slice(0, half))
+        group_x(nc.vector.tensor_copy, slice(half, share))
+        group_x(nc.scalar.copy, slice(share, SIZE))
+        w1_flipped = [flip([w1_natural[:, i, :]], weight_banks[i]) for i in range(2)]
+        b2_spread = psum.tile([P, SIZE], BF16, tag=weight_banks[3])
         nc.tensor.matmul(out=b2_spread[:], lhsT=ones[:], rhs=b2_rows[:], start=True, stop=True)
-        w1_flipped.extend([flip(w1_natural[:, i, :], weight_banks[i]) for i in range(2, TILES)])
-        fetch(nc.scalar.copy, w1_flipped[0], w1_grouped[:, 0, :])
-        fetch(nc.scalar.copy, w1_flipped[1], w1_grouped[:, 1, :])
-        nc.scalar.copy(out=b2_all[:], in_=b2_spread[:])
-        for t in range(PACK - 1):
-            quantise_x(t)
-        quantise_w1(0)
-        quantise_x(PACK - 1)
-        quantise_w1(1)
-        fetch(nc.vector.tensor_copy, w1_flipped[2], w1_grouped[:, 2, :])
-        fetch(nc.vector.tensor_copy, w1_flipped[3], w1_grouped[:, 3, :])
-        quantise_w1(2)
-        quantise_w1(3)
+        w1_flipped.append(flip([w1_natural[:, 2, :], w1_natural[:, 3, :]], weight_banks[2]))
+        keep_clock(1)
+        fetch(nc.scalar.copy, w1_flipped[0], w1_grouped[:, 0:1, :])
+        fetch(nc.scalar.copy, w1_flipped[1], w1_grouped[:, 1:2, :])
+        quantise_x(slice(0, half))
+        quantise_x(slice(half, SIZE))
+        quantise_w1(slice(0, 1))
+        quantise_w1(slice(1, 2))
+        fetch(nc.vector.tensor_copy, w1_flipped[2], w1_grouped[:, 2:4, :])
+        quantise_w1(slice(2, 4))
 
         z0 = first_product(0, 2)
         z1 = first_product(1, 1)
-        w2_flipped = [flip(w2_natural[:, i, :], weight_banks[i]) for i in range(TILES)]
+        w2_flipped = [
+            flip([w2_natural[:, 0, :], w2_natural[:, 1, :]], weight_banks[1]),
+            flip([w2_natural[:, 2, :], w2_natural[:, 3, :]], weight_banks[0]),
+        ]
         u0 = gelu(0, z0, 2)
-        u0_flipped = flip(u0[:], chunk_banks[0])
+        u0_flipped = flip([u0[:]], chunk_banks[0])
         z2 = first_product(2, 1)
-        z3 = first_product(3, 1)
-        fetch(nc.vector.tensor_copy, w2_flipped[0], w2_grouped[:, 0, :])
-        fetch(nc.vector.tensor_copy, w2_flipped[1], w2_grouped[:, 1, :])
-        fetch(nc.scalar.copy, w2_flipped[2], w2_grouped[:, 2, :])
-        fetch(nc.scalar.copy, w2_flipped[3], w2_grouped[:, 3, :])
+        fetch(nc.vector.tensor_copy, w2_flipped[0], w2_grouped[:, 0:2, :])
         u1 = gelu(1, z1, 1)
+        u1_flipped = flip([u1[:]], chunk_banks[1])
+        z3 = first_product(3, 1)
+        fetch(nc.scalar.copy, w2_flipped[1], w2_grouped[:, 2:4, :])
         u2 = gelu(2, z2, 1)
+        fetch(nc.scalar.copy, u1_flipped, u_grouped[:, 1:2, :])
         u3 = gelu(3, z3, 1)
 
-        fetch(nc.vector.tensor_copy, u0_flipped, u_grouped[:, 0, :])
+        fetch(nc.vector.tensor_copy, u0_flipped, u_grouped[:, 0:1, :])
         quantise(w2_codes, w2_scales, w2_grouped, slice(0, TILES))
         quantise_u(0)
-        u1_flipped = flip(u1[:], chunk_banks[1])
-        fetch(nc.vector.tensor_copy, u1_flipped, u_grouped[:, 1, :])
-        u2_flipped = flip(u2[:], chunk_banks[2])
-        fetch(nc.scalar.copy, u2_flipped, u_grouped[:, 2, :])
-        y0 = second_product(0)
-        u3_flipped = flip(u3[:], chunk_banks[3])
-        fetch(nc.scalar.copy, u3_flipped, u_grouped[:, 3, :])
+        nc.vector.tensor_copy(out=b2_all[:], in_=b2_spread[:])
         quantise_u(1)
+        u2_flipped = flip([u2[:]], chunk_banks[2])
+        fetch(nc.scalar.copy, u2_flipped, u_grouped[:, 2:3, :])
+        y0 = second_product(0)
+        u3_flipped = flip([u3[:]], chunk_banks[3])
+        fetch(nc.scalar.copy, u3_flipped, u_grouped[:, 3:4, :])
         y1 = second_product(1)
         add_b2_and_store(0, y0, 1)
         quantise_u(2)

@@ -50,7 +50,10 @@ def tile_getspatialgatingweights_pa_s_kernel(tc, x_norm, w1_u, b1_u, w2, b2, out
         nc.sync.dma_start(out=w1_natural[:, 1, :], in_=w1_rows[:, 1, :])
         nc.sync.dma_start(out=w1_natural[:, 2:4, :], in_=w1_rows[:, 2:4, :])
         w2_natural = keep.tile([P, TILES, SIZE], BF16)
-        nc.sync.dma_start(out=w2_natural[:], in_=w2.rearrange("(r i) g -> r i g", i=TILES))
+        nc.sync.dma_start(
+            out=w2_natural[:].rearrange("r (a i) g -> r a i g", a=HALVES),
+            in_=w2.rearrange("(a r i) g -> r a i g", a=HALVES, i=PAIR),
+        )
 
         constant = keep.tile([P, P], F32)
         nc.vector.memset(constant[:], 0.0)
@@ -120,60 +123,53 @@ def tile_getspatialgatingweights_pa_s_kernel(tc, x_norm, w1_u, b1_u, w2, b2, out
         def quantise_w1(tiles):
             quantise(w1_codes, w1_scales, w1_grouped, tiles)
 
+        def quantise_w2(tiles):
+            quantise(w2_codes, w2_scales, w2_grouped, tiles)
+
         def quantise_u(m):
             quantise(u_codes, u_scales, u_grouped, slice(m, m + 1))
 
-        def first_product(m, pieces):
-            z = psum.tile([P, SIZE], F32, tag=chunk_banks[m])
-            width = SIZE // pieces
-            for n in range(pieces):
-                cells = slice(n * width, (n + 1) * width)
-                nc.tensor.matmul_mx(
-                    out=z[:, cells],
-                    lhsT=w1_codes[:, m, :].bitcast(FP8X4),
-                    lhsT_scale=w1_scales[:, m, :],
-                    rhs=x_codes[:, cells].bitcast(FP8X4),
-                    rhs_scale=x_scales[:, cells],
-                    start=True,
-                    stop=True,
-                )
+        def first_product(m, cells, bank):
+            z = psum.tile([P, cells.stop - cells.start], F32, tag=bank)
+            nc.tensor.matmul_mx(
+                out=z[:],
+                lhsT=w1_codes[:, m, :].bitcast(FP8X4),
+                lhsT_scale=w1_scales[:, m, :],
+                rhs=x_codes[:, cells].bitcast(FP8X4),
+                rhs_scale=x_scales[:, cells],
+                start=True,
+                stop=True,
+            )
             return z
 
-        def gelu(m, z, pieces):
-            u = stage.tile([P, SIZE], BF16, tag="u")
-            width = SIZE // pieces
-            for n in range(pieces):
-                cells = slice(n * width, (n + 1) * width)
-                nc.scalar.activation(out=u[:, cells], in_=z[:, cells], func=GELU, bias=b1_columns[:, m : m + 1])
-            return u
+        def gelu(m, z, u):
+            nc.scalar.activation(out=u, in_=z[:], func=GELU, bias=b1_columns[:, m : m + 1])
 
-        def second_product(m):
-            y = psum.tile([P, SIZE], F32, tag=chunk_banks[m])
+        def second_product(m, tiles, bank):
+            y = psum.tile([P, tiles.stop - tiles.start, P], F32, tag=bank)
             nc.tensor.matmul_mx(
-                out=y[:],
+                out=y[:].rearrange("k i r -> k (i r)"),
                 lhsT=u_codes[:, m, :].bitcast(FP8X4),
                 lhsT_scale=u_scales[:, m, :],
-                rhs=w2_codes[:].rearrange("p i r -> p (i r)").bitcast(FP8X4),
-                rhs_scale=w2_scales[:].rearrange("p i r -> p (i r)"),
+                rhs=w2_codes[:, tiles, :].rearrange("p i r -> p (i r)").bitcast(FP8X4),
+                rhs_scale=w2_scales[:, tiles, :].rearrange("p i r -> p (i r)"),
                 start=True,
                 stop=True,
             )
             return y
 
-        def add_b2_and_store(m, y, pieces):
-            result = stage.tile([P, SIZE], F32, tag="result")
-            y_sorted = y[:].rearrange("k (i r) -> k r i", i=TILES)
-            width = P // pieces
-            for n in range(pieces):
-                r = slice(n * width, (n + 1) * width)
-                cells = slice(n * width * TILES, (n + 1) * width * TILES)
-                nc.vector.tensor_tensor(
-                    out=result[:, cells].rearrange("k (r i) -> k r i", i=TILES),
-                    in0=y_sorted[:, r, :],
-                    in1=b2_all[:, cells].rearrange("k (r i) -> k r i", i=TILES),
-                    op=ADD,
-                )
-                nc.sync.dma_start(out=out_rows[m][:, cells], in_=result[:, cells])
+        def add_b2_and_store(m, a, y):
+            cells = slice(a * SIZE // HALVES, (a + 1) * SIZE // HALVES)
+            nc.vector.tensor_tensor(
+                out=results[m][:, cells].rearrange("k (r i) -> k r i", i=PAIR),
+                in0=y.rearrange("k i r -> k r i"),
+                in1=b2_all[:, cells].rearrange("k (r i) -> k r i", i=PAIR),
+                op=ADD,
+            )
+            nc.sync.dma_start(out=out_rows[m][:, cells], in_=results[m][:, cells])
+
+        u = [keep.tile([P, SIZE], BF16, name="u%d" % m) for m in range(TILES)]
+        results = [keep.tile([P, SIZE], F32, name="result%d" % m) for m in range(TILES)]
 
         half = SIZE // 2
         share = SIZE * 5 // 8
@@ -187,6 +183,7 @@ def tile_getspatialgatingweights_pa_s_kernel(tc, x_norm, w1_u, b1_u, w2, b2, out
         keep_clock(1)
         fetch(nc.scalar.copy, w1_flipped[0], w1_grouped[:, 0:1, :])
         fetch(nc.scalar.copy, w1_flipped[1], w1_grouped[:, 1:2, :])
+        nc.scalar.copy(out=b2_all[:], in_=b2_spread[:])
         quantise_x(slice(0, half))
         quantise_x(slice(half, SIZE))
         quantise_w1(slice(0, 1))
@@ -194,40 +191,48 @@ def tile_getspatialgatingweights_pa_s_kernel(tc, x_norm, w1_u, b1_u, w2, b2, out
         fetch(nc.vector.tensor_copy, w1_flipped[2], w1_grouped[:, 2:4, :])
         quantise_w1(slice(2, 4))
 
-        z0 = first_product(0, 2)
-        z1 = first_product(1, 1)
+        low, high, whole = slice(0, half), slice(half, SIZE), slice(0, SIZE)
+        z0_low = first_product(0, low, chunk_banks[0])
+        z0_high = first_product(0, high, chunk_banks[3])
+        z1 = first_product(1, whole, chunk_banks[1])
         w2_flipped = [
             flip([w2_natural[:, 0, :], w2_natural[:, 1, :]], weight_banks[1]),
             flip([w2_natural[:, 2, :], w2_natural[:, 3, :]], weight_banks[0]),
         ]
-        u0 = gelu(0, z0, 2)
-        u0_flipped = flip([u0[:]], chunk_banks[0])
-        z2 = first_product(2, 1)
+        gelu(0, z0_low, u[0][:, low])
+        gelu(0, z0_high, u[0][:, high])
+        u0_flipped = flip([u[0][:]], chunk_banks[0])
+        z2 = first_product(2, whole, chunk_banks[2])
+        gelu(1, z1, u[1][:])
+        u1_flipped = flip([u[1][:]], chunk_banks[1])
+        z3 = first_product(3, whole, chunk_banks[3])
         fetch(nc.vector.tensor_copy, w2_flipped[0], w2_grouped[:, 0:2, :])
-        u1 = gelu(1, z1, 1)
-        u1_flipped = flip([u1[:]], chunk_banks[1])
-        z3 = first_product(3, 1)
         fetch(nc.scalar.copy, w2_flipped[1], w2_grouped[:, 2:4, :])
-        u2 = gelu(2, z2, 1)
-        fetch(nc.scalar.copy, u1_flipped, u_grouped[:, 1:2, :])
-        u3 = gelu(3, z3, 1)
+        gelu(2, z2, u[2][:])
+        gelu(3, z3, u[3][:])
 
         fetch(nc.vector.tensor_copy, u0_flipped, u_grouped[:, 0:1, :])
-        quantise(w2_codes, w2_scales, w2_grouped, slice(0, TILES))
+        quantise_w2(slice(0, 2))
         quantise_u(0)
-        nc.vector.tensor_copy(out=b2_all[:], in_=b2_spread[:])
-        quantise_u(1)
-        u2_flipped = flip([u2[:]], chunk_banks[2])
+        quantise_w2(slice(2, 4))
+        fetch(nc.vector.tensor_copy, u1_flipped, u_grouped[:, 1:2, :])
+        y0_low = second_product(0, slice(0, 2), chunk_banks[0])
+        u2_flipped = flip([u[2][:]], chunk_banks[2])
         fetch(nc.scalar.copy, u2_flipped, u_grouped[:, 2:3, :])
-        y0 = second_product(0)
-        u3_flipped = flip([u3[:]], chunk_banks[3])
+        y0_high = second_product(0, slice(2, 4), weight_banks[2])
+        add_b2_and_store(0, 0, y0_low[:])
+        quantise_u(1)
+        u3_flipped = flip([u[3][:]], chunk_banks[3])
         fetch(nc.scalar.copy, u3_flipped, u_grouped[:, 3:4, :])
-        y1 = second_product(1)
-        add_b2_and_store(0, y0, 1)
+        y1 = second_product(1, slice(0, 4), chunk_banks[1])
+        add_b2_and_store(0, 1, y0_high[:])
         quantise_u(2)
-        y2 = second_product(2)
-        add_b2_and_store(1, y1, 1)
+        y2 = second_product(2, slice(0, 4), chunk_banks[2])
+        add_b2_and_store(1, 0, y1[:, 0:2, :])
         quantise_u(3)
-        y3 = second_product(3)
-        add_b2_and_store(2, y2, 1)
-        add_b2_and_store(3, y3, 2)
+        y3 = second_product(3, slice(0, 4), chunk_banks[3])
+        add_b2_and_store(1, 1, y1[:, 2:4, :])
+        add_b2_and_store(2, 0, y2[:, 0:2, :])
+        add_b2_and_store(2, 1, y2[:, 2:4, :])
+        add_b2_and_store(3, 0, y3[:, 0:2, :])
+        add_b2_and_store(3, 1, y3[:, 2:4, :])

@@ -50,10 +50,9 @@ def tile_getspatialgatingweights_pa_s_kernel(tc, x_norm, w1_u, b1_u, w2, b2, out
         nc.sync.dma_start(out=w1_natural[:, 1, :], in_=w1_rows[:, 1, :])
         nc.sync.dma_start(out=w1_natural[:, 2:4, :], in_=w1_rows[:, 2:4, :])
         w2_natural = keep.tile([P, TILES, SIZE], BF16)
-        nc.sync.dma_start(
-            out=w2_natural[:].rearrange("r (a i) g -> r a i g", a=HALVES),
-            in_=w2.rearrange("(a r i) g -> r a i g", a=HALVES, i=PAIR),
-        )
+        w2_rows = w2.rearrange("(a r i) g -> a r i g", a=HALVES, i=PAIR)
+        for a in range(HALVES):
+            nc.sync.dma_start(out=w2_natural[:, a * PAIR : (a + 1) * PAIR, :], in_=w2_rows[a])
 
         constant = keep.tile([P, P], F32)
         nc.vector.memset(constant[:], 0.0)
@@ -224,15 +223,18 @@ def tile_getspatialgatingweights_pa_s_kernel(tc, x_norm, w1_u, b1_u, w2, b2, out
         quantise_u(1)
         u3_flipped = flip([u[3][:]], chunk_banks[3])
         fetch(nc.scalar.copy, u3_flipped, u_grouped[:, 3:4, :])
-        y1 = second_product(1, slice(0, 4), chunk_banks[1])
+        y1_low = second_product(1, slice(0, 2), chunk_banks[1])
+        y1_high = second_product(1, slice(2, 4), weight_banks[3])
         add_b2_and_store(0, 1, y0_high[:])
         quantise_u(2)
-        y2 = second_product(2, slice(0, 4), chunk_banks[2])
-        add_b2_and_store(1, 0, y1[:, 0:2, :])
+        y2_low = second_product(2, slice(0, 2), chunk_banks[2])
+        y2_high = second_product(2, slice(2, 4), weight_banks[1])
+        add_b2_and_store(1, 0, y1_low[:])
         quantise_u(3)
-        y3 = second_product(3, slice(0, 4), chunk_banks[3])
-        add_b2_and_store(1, 1, y1[:, 2:4, :])
-        add_b2_and_store(2, 0, y2[:, 0:2, :])
-        add_b2_and_store(2, 1, y2[:, 2:4, :])
-        add_b2_and_store(3, 0, y3[:, 0:2, :])
-        add_b2_and_store(3, 1, y3[:, 2:4, :])
+        y3_low = second_product(3, slice(0, 2), chunk_banks[3])
+        y3_high = second_product(3, slice(2, 4), weight_banks[0])
+        add_b2_and_store(1, 1, y1_high[:])
+        add_b2_and_store(2, 0, y2_low[:])
+        add_b2_and_store(2, 1, y2_high[:])
+        add_b2_and_store(3, 0, y3_low[:])
+        add_b2_and_store(3, 1, y3_high[:])

@@ -42,13 +42,13 @@ def tile_getspatialgatingweights_pa_s_kernel(tc, x_norm, w1_u, b1_u, w2, b2, out
         w1_rows = w1_u.rearrange("(r i) c -> r i c", i=TILES)
         w1_natural = keep.tile([P, TILES, SIZE], BF16)
         nc.sync.dma_start(out=w1_natural[:, 0, :], in_=w1_rows[:, 0, :])
-        b1_columns = keep.tile([P, TILES], BF16)
-        nc.sync.dma_start(out=b1_columns[:], in_=b1_u.rearrange("(k m) -> k m", m=TILES))
         b2_rows = keep.tile([P, SIZE], BF16)
         nc.gpsimd.memset(b2_rows[:].bitcast(F32), 0.0)
         nc.sync.dma_start(out=b2_rows[0:1, :], in_=b2.unsqueeze(0))
         nc.sync.dma_start(out=w1_natural[:, 1, :], in_=w1_rows[:, 1, :])
         nc.sync.dma_start(out=w1_natural[:, 2:4, :], in_=w1_rows[:, 2:4, :])
+        b1_columns = keep.tile([P, TILES], BF16)
+        nc.sync.dma_start(out=b1_columns[:], in_=b1_u.rearrange("(k m) -> k m", m=TILES))
         w2_natural = keep.tile([P, TILES, SIZE], BF16)
         w2_rows = w2.rearrange("(a r i) g -> a r i g", a=HALVES, i=PAIR)
         for a in range(HALVES):

from contextlib import ExitStack

import concourse.mybir as mybir
from concourse.masks import make_identity

F32 = mybir.dt.float32
BF16 = mybir.dt.bfloat16
U32 = mybir.dt.uint32
U8 = mybir.dt.uint8
FP8X4 = mybir.dt.float8_e4m3fn_x4
ADD = mybir.AluOpType.add
GELU = mybir.ActivationFunctionType.Gelu

P = 128
PACK = 4
HALVES = 2
PAIR = 2
SIZE = P * PACK
TILES = SIZE // P

FLOPS = 2 * 2 * SIZE * SIZE * SIZE


def tile_getspatialgatingweights_pa_s_kernel(tc, x_norm, w1_u, b1_u, w2, b2, out):
    nc = tc.nc
    x_rows = x_norm.rearrange("n c d h w -> (n c) (d h w)")
    out_rows = out.rearrange("n (k m) d h w -> m (n k) (d h w)", m=TILES)

    with ExitStack() as ctx:
        ctx.enter_context(tc.manual_schedule())
        keep = ctx.enter_context(tc.tile_pool(name="keep", bufs=1))
        stage = ctx.enter_context(tc.tile_pool(name="stage", bufs=TILES))
        psum = ctx.enter_context(tc.psum_pool(name="psum", bufs=1))
        weight_banks = ["weight%d" % i for i in range(TILES)]
        chunk_banks = ["chunk%d" % m for m in range(TILES)]

        x_raw = keep.tile([P, PACK, SIZE], BF16)
        nc.sync.dma_start(
            out=x_raw[:].rearrange("p (h e) v -> p h e v", h=HALVES),
            in_=x_rows.rearrange("(h p e) v -> p h e v", h=HALVES, e=PAIR),
        )
        w1_rows = w1_u.rearrange("(r i) c -> r i c", i=TILES)
        w1_natural = keep.tile([P, TILES, SIZE], BF16)
        nc.sync.dma_start(out=w1_natural[:, 0, :], in_=w1_rows[:, 0, :])
        b2_rows = keep.tile([P, SIZE], BF16)
        nc.gpsimd.memset(b2_rows[:].bitcast(F32), 0.0)
        nc.sync.dma_start(out=b2_rows[0:1, :], in_=b2.unsqueeze(0))
        nc.sync.dma_start(out=w1_natural[:, 1, :], in_=w1_rows[:, 1, :])
        nc.sync.dma_start(out=w1_natural[:, 2:4, :], in_=w1_rows[:, 2:4, :])
        b1_columns = keep.tile([P, TILES], BF16)
        nc.sync.dma_start(out=b1_columns[:], in_=b1_u.rearrange("(k m) -> k m", m=TILES))
        w2_natural = keep.tile([P, TILES, SIZE], BF16)
        w2_rows = w2.rearrange("(a r i) g -> a r i g", a=HALVES, i=PAIR)
        for a in range(HALVES):
            nc.sync.dma_start(out=w2_natural[:, a * PAIR : (a + 1) * PAIR, :], in_=w2_rows[a])

        constant = keep.tile([P, P], F32)
        nc.vector.memset(constant[:], 0.0)
        unread = psum.tile([P, P], F32, tag=chunk_banks[3])

        def keep_clock(count):
            for n in range(count):
                nc.tensor.matmul(out=unread[:], lhsT=constant[:], rhs=constant[:], start=True, stop=True)

        keep_clock(4)
        ones = keep.tile([P, P], BF16)
        nc.vector.memset(ones[:], 1.0)
        identity = keep.tile([P, P], F32)
        make_identity(nc, identity[:])
        zero_column = keep.tile([P, 1], F32)
        nc.vector.memset(zero_column[:], 0.0)
        unused_column = keep.tile([P, 1], F32)
        nc.scalar.activation(out=unused_column[:], in_=zero_column[:], func=GELU)

        x_grouped = keep.tile([P, SIZE, PACK], BF16, align_bytes=64)
        x_codes = keep.tile([P, SIZE], U32, align_bytes=64)
        x_scales = keep.tile([P, SIZE], U8, align_bytes=64)

        def group_x(engine_copy, columns):
            engine_copy(out=x_grouped[:, columns, :], in_=x_raw[:, :, columns].rearrange("p j v -> p v j"))

        def quantise_x(columns):
            nc.vector.quantize_mx(
                out=x_codes[:, columns].bitcast(FP8X4),
                scales=x_scales[:, columns],
                in_=x_grouped[:, columns, :].rearrange("p v j -> p (v j)"),
            )

        def flip(natural, bank):
            tiles = len(natural)
            flipped = psum.tile([P, tiles, HALVES, P], F32, tag=bank)
            for i in range(tiles):
                words = natural[i].bitcast(F32).rearrange("r (h p) -> r h p", h=HALVES)
                for h in range(HALVES):
                    nc.tensor.transpose(out=flipped[:, i, h, :], in_=words[:, h, :], identity=identity[:])
            return flipped

        def fetch(engine_copy, flipped, grouped):
            engine_copy(
                out=grouped.rearrange("p i c -> p (i c)").bitcast(F32).rearrange("p (i r h) -> p i r h", r=P, h=HALVES),
                in_=flipped[:].rearrange("p i h r -> p i r h"),
            )

        w1_grouped = keep.tile([P, TILES, SIZE], BF16, align_bytes=64)
        w1_codes = keep.tile([P, TILES, P], U32, align_bytes=64)
        w1_scales = keep.tile([P, TILES, P], U8, align_bytes=64)
        w2_grouped = keep.tile([P, TILES, SIZE], BF16, align_bytes=64)
        w2_codes = keep.tile([P, TILES, P], U32, align_bytes=64)
        w2_scales = keep.tile([P, TILES, P], U8, align_bytes=64)
        u_grouped = keep.tile([P, TILES, SIZE], BF16, align_bytes=64)
        u_codes = keep.tile([P, TILES, P], U32, align_bytes=64)
        u_scales = keep.tile([P, TILES, P], U8, align_bytes=64)
        b2_all = keep.tile([P, SIZE], BF16)

        def quantise(codes, scales, grouped, tiles):
            nc.vector.quantize_mx(
                out=codes[:, tiles, :].rearrange("p i r -> p (i r)").bitcast(FP8X4),
                scales=scales[:, tiles, :].rearrange("p i r -> p (i r)"),
                in_=grouped[:, tiles, :].rearrange("p i c -> p (i c)"),
            )

        def quantise_w1(tiles):
            quantise(w1_codes, w1_scales, w1_grouped, tiles)

        def quantise_w2(tiles):
            quantise(w2_codes, w2_scales, w2_grouped, tiles)

        def quantise_u(m):
            quantise(u_codes, u_scales, u_grouped, slice(m, m + 1))

        def first_product(m, cells, bank):
            z = psum.tile([P, cells.stop - cells.start], F32, tag=bank)
            nc.tensor.matmul_mx(
                out=z[:],
                lhsT=w1_codes[:, m, :].bitcast(FP8X4),
                lhsT_scale=w1_scales[:, m, :],
                rhs=x_codes[:, cells].bitcast(FP8X4),
                rhs_scale=x_scales[:, cells],
                start=True,
                stop=True,
            )
            return z

        def gelu(m, z, u):
            nc.scalar.activation(out=u, in_=z[:], func=GELU, bias=b1_columns[:, m : m + 1])

        def second_product(m, tiles, bank):
            y = psum.tile([P, tiles.stop - tiles.start, P], F32, tag=bank)
            nc.tensor.matmul_mx(
                out=y[:].rearrange("k i r -> k (i r)"),
                lhsT=u_codes[:, m, :].bitcast(FP8X4),
                lhsT_scale=u_scales[:, m, :],
                rhs=w2_codes[:, tiles, :].rearrange("p i r -> p (i r)").bitcast(FP8X4),
                rhs_scale=w2_scales[:, tiles, :].rearrange("p i r -> p (i r)"),
                start=True,
                stop=True,
            )
            return y

        def add_b2_and_store(m, a, y):
            cells = slice(a * SIZE // HALVES, (a + 1) * SIZE // HALVES)
            nc.vector.tensor_tensor(
                out=results[m][:, cells].rearrange("k (r i) -> k r i", i=PAIR),
                in0=y.rearrange("k i r -> k r i"),
                in1=b2_all[:, cells].rearrange("k (r i) -> k r i", i=PAIR),
                op=ADD,
            )
            nc.sync.dma_start(out=out_rows[m][:, cells], in_=results[m][:, cells])

        u = [keep.tile([P, SIZE], BF16, name="u%d" % m) for m in range(TILES)]
        results = [keep.tile([P, SIZE], F32, name="result%d" % m) for m in range(TILES)]

        half = SIZE // 2
        share = SIZE * 5 // 8
        group_x(nc.vector.tensor_copy, slice(0, half))
        group_x(nc.vector.tensor_copy, slice(half, share))
        group_x(nc.scalar.copy, slice(share, SIZE))
        w1_flipped = [flip([w1_natural[:, i, :]], weight_banks[i]) for i in range(2)]
        b2_spread = psum.tile([P, SIZE], BF16, tag=weight_banks[3])
        nc.tensor.matmul(out=b2_spread[:], lhsT=ones[:], rhs=b2_rows[:], start=True, stop=True)
        w1_flipped.append(flip([w1_natural[:, 2, :], w1_natural[:, 3, :]], weight_banks[2]))
        keep_clock(1)
        fetch(nc.scalar.copy, w1_flipped[0], w1_grouped[:, 0:1, :])
        fetch(nc.scalar.copy, w1_flipped[1], w1_grouped[:, 1:2, :])
        nc.scalar.copy(out=b2_all[:], in_=b2_spread[:])
        quantise_x(slice(0, half))
        quantise_x(slice(half, SIZE))
        quantise_w1(slice(0, 1))
        quantise_w1(slice(1, 2))
        fetch(nc.vector.tensor_copy, w1_flipped[2], w1_grouped[:, 2:4, :])
        quantise_w1(slice(2, 4))

        low, high, whole = slice(0, half), slice(half, SIZE), slice(0, SIZE)
        z0_low = first_product(0, low, chunk_banks[0])
        z0_high = first_product(0, high, chunk_banks[3])
        z1 = first_product(1, whole, chunk_banks[1])
        w2_flipped = [
            flip([w2_natural[:, 0, :], w2_natural[:, 1, :]], weight_banks[1]),
            flip([w2_natural[:, 2, :], w2_natural[:, 3, :]], weight_banks[0]),
        ]
        gelu(0, z0_low, u[0][:, low])
        gelu(0, z0_high, u[0][:, high])
        u0_flipped = flip([u[0][:]], chunk_banks[0])
        z2 = first_product(2, whole, chunk_banks[2])
        gelu(1, z1, u[1][:])
        u1_flipped = flip([u[1][:]], chunk_banks[1])
        z3 = first_product(3, whole, chunk_banks[3])
        fetch(nc.vector.tensor_copy, w2_flipped[0], w2_grouped[:, 0:2, :])
        fetch(nc.scalar.copy, w2_flipped[1], w2_grouped[:, 2:4, :])
        gelu(2, z2, u[2][:])
        gelu(3, z3, u[3][:])

        fetch(nc.vector.tensor_copy, u0_flipped, u_grouped[:, 0:1, :])
        quantise_w2(slice(0, 2))
        quantise_u(0)
        quantise_w2(slice(2, 4))
        fetch(nc.vector.tensor_copy, u1_flipped, u_grouped[:, 1:2, :])
        y0_low = second_product(0, slice(0, 2), chunk_banks[0])
        u2_flipped = flip([u[2][:]], chunk_banks[2])
        fetch(nc.scalar.copy, u2_flipped, u_grouped[:, 2:3, :])
        y0_high = second_product(0, slice(2, 4), weight_banks[2])
        add_b2_and_store(0, 0, y0_low[:])
        quantise_u(1)
        u3_flipped = flip([u[3][:]], chunk_banks[3])
        fetch(nc.scalar.copy, u3_flipped, u_grouped[:, 3:4, :])
        y1_low = second_product(1, slice(0, 2), chunk_banks[1])
        y1_high = second_product(1, slice(2, 4), weight_banks[3])
        add_b2_and_store(0, 1, y0_high[:])
        quantise_u(2)
        y2_low = second_product(2, slice(0, 2), chunk_banks[2])
        y2_high = second_product(2, slice(2, 4), weight_banks[1])
        add_b2_and_store(1, 0, y1_low[:])
        quantise_u(3)
        y3_low = second_product(3, slice(0, 2), chunk_banks[3])
        y3_high = second_product(3, slice(2, 4), weight_banks[0])
        add_b2_and_store(1, 1, y1_high[:])
        add_b2_and_store(2, 0, y2_low[:])
        add_b2_and_store(2, 1, y2_high[:])
        add_b2_and_store(3, 0, y3_low[:])
        add_b2_and_store(3, 1, y3_high[:])
